import numpy as np
import ml_dtypes

BF16 = ml_dtypes.bfloat16


def bf(x):
    return np.asarray(x, np.float32).astype(BF16)


def f32(x):
    return np.asarray(x, np.float32)


def f64(x):
    return np.asarray(x).astype(np.float64)


def striped(idx):
    return np.tile(idx.reshape(-1, 16).T, (8, 1))


C, F, O, P, Z, S, H, K, N = 256, 256, 128, 128, 512, 4096, 2048, 4, 8192


def mlp2(h, wa, ba, wb, bb):
    u = np.maximum(f64(wa).T @ h + f64(ba), 0.0)
    return np.maximum(f64(wb).T @ u + f64(bb), 0.0)


def setup_inputs():
    inp = {"x": f32(np.random.standard_normal((C, S))), "xd": f32(np.random.standard_normal((C, N))), "edge_attr": bf(np.random.standard_normal((P, N)))}
    for t in ("1", "3", "4"):
        inp["w" + t + "a"] = bf(np.random.standard_normal((C, F)) / np.sqrt(C))
        inp["b" + t + "a"] = f32(0.1 * np.random.standard_normal((F, 1)))
        inp["w" + t + "b"] = bf(np.random.standard_normal((F, O)) / np.sqrt(F))
        inp["b" + t + "b"] = f32(0.1 * np.random.standard_normal((O, 1)))
    inp["wf"] = bf(np.random.standard_normal((Z, O)) / np.sqrt(Z))
    inp["ws"] = f32(2.0 * np.random.standard_normal((O, 1)))
    inp["bfin"] = f32(0.1 * np.random.standard_normal((O, 1)))
    inp["offs"] = striped(np.concatenate([np.random.permutation(S)[:H] for _ in range(K)]))
    return inp


def reference(x, xd, edge_attr, w1a, b1a, w1b, b1b, w3a, b3a, w3b, b3b, w4a, b4a, w4b, b4b, wf, ws, bfin, offs):
    idx = offs[:16].T.reshape(-1)
    xdv = f64(xd)
    xs = f64(x)[:, idx]
    d = xs + (-xdv)
    p = xs * xdv
    y1 = mlp2(xs, w1a, b1a, w1b, b1b)
    y3 = mlp2(d, w3a, b3a, w3b, b3b)
    y4 = mlp2(p, w4a, b4a, w4b, b4b)
    ns = np.sqrt(np.sum(xs * xs, axis=0, keepdims=True))
    nd = np.sqrt(np.sum(xdv * xdv, axis=0, keepdims=True))
    cs = np.sum(p, axis=0, keepdims=True) / (ns * nd)
    z = np.concatenate([y1, y3, y4, f64(edge_attr)], axis=0)
    return np.tanh(f64(wf).T @ z + f64(ws) * cs + f64(bfin))

@@ -1,0 +1,212 @@
+import concourse.mybir as mybir
+from concourse.masks import make_identity
+
+F32 = mybir.dt.float32
+BF16 = mybir.dt.bfloat16
+U16 = mybir.dt.uint16
+ALU = mybir.AluOpType
+ACT = mybir.ActivationFunctionType
+
+P = 128
+C, F, O, Z, S, N = 256, 256, 128, 512, 4096, 8192
+CB = C // P
+FB = F // P
+ZB = Z // P
+W = 512
+CHUNKS = N // W
+GROUP = 4
+QUAD = P // GROUP
+FINAL_LAG = GROUP
+
+FLOPS = 2 * N * (3 * C * F + 3 * F * O + Z * O)
+
+
+def tile_edgeattrs_b_kernel(
+    tc, x, xd, edge_attr,
+    w1a, b1a, w1b, b1b, w3a, b3a, w3b, b3b, w4a, b4a, w4b, b4b,
+    wf, ws, bfin, offs, out,
+):
+    nc = tc.nc
+    with (
+        tc.tile_pool(name="held", bufs=1) as held,
+        tc.tile_pool(name="stream", bufs=3) as stream,
+        tc.tile_pool(name="hidden", bufs=6) as hidden,
+        tc.tile_pool(name="late", bufs=FINAL_LAG + 2) as late,
+        tc.tile_pool(name="cosine", bufs=2) as cosine,
+        tc.psum_pool(name="sums", bufs=1) as sums,
+        tc.psum_pool(name="banks", bufs=5) as banks,
+    ):
+        def load(queue, shape, dtype, source, name):
+            tile = held.tile(shape, dtype, name=name)
+            queue.dma_start(tile[:], source)
+            return tile
+
+        offsets = held.tile([P, N // 16], U16, name="offsets")
+        nc.sync.dma_start(offsets[:], offs)
+        xd_blocks = xd.rearrange("(cb p) n -> p cb n", p=P)
+        xd_tiles = {}
+
+        def fetch_xd(c):
+            xd_t = stream.tile([P, CB, W], F32, name="xd_t", bufs=4)
+            nc.sync.dma_start(xd_t[:], xd_blocks[:, :, c * W:(c + 1) * W])
+            xd_tiles[c] = xd_t
+
+        fetch_xd(0)
+        table = [
+            load(nc.sync, [P, S], F32, x[cb * P:(cb + 1) * P, :], "table%d" % cb)
+            for cb in range(CB)
+        ]
+        fetch_xd(1)
+
+        def first_weight(w, name):
+            return load(nc.scalar, [P, CB, F], BF16, w.rearrange("(cb p) f -> p cb f", p=P), name)
+
+        def second_weight(w, name):
+            return load(nc.scalar, [P, FB, O], BF16, w.rearrange("(fb p) o -> p fb o", p=P), name)
+
+        def bias(b, blocks, name):
+            return load(nc.scalar, [P, blocks], F32, b.rearrange("(a p) o -> p (a o)", p=P), name)
+
+        branches = (
+            ("xs", first_weight(w1a, "w1a_t"), bias(b1a, FB, "b1a_t"),
+             second_weight(w1b, "w1b_t"), bias(b1b, 1, "b1b_t")),
+            ("d", first_weight(w3a, "w3a_t"), bias(b3a, FB, "b3a_t"),
+             second_weight(w3b, "w3b_t"), bias(b3b, 1, "b3b_t")),
+            ("p", first_weight(w4a, "w4a_t"), bias(b4a, FB, "b4a_t"),
+             second_weight(w4b, "w4b_t"), bias(b4b, 1, "b4b_t")),
+        )
+        wf_t = load(nc.scalar, [P, ZB, O], BF16, wf.rearrange("(zb p) o -> p zb o", p=P), "wf_t")
+        bfin_t = bias(bfin, 1, "bfin_t")
+
+        ones = held.tile([P, QUAD], BF16, name="ones")
+        nc.vector.memset(ones[:], 1.0)
+
+        identity = held.tile([P, P], F32, name="identity")
+        make_identity(nc, identity[:])
+        ws_rows = load(nc.scalar, [P, O], F32,
+                       ws.rearrange("o one -> (o one)").partition_broadcast(P), "ws_rows")
+        ws_high = held.tile([P, O], BF16, name="ws_high")
+        nc.vector.tensor_copy(ws_high[:], ws_rows[:])
+        ws_low = held.tile([P, O], BF16, name="ws_low")
+        nc.vector.tensor_tensor(ws_low[:], ws_rows[:], ws_high[:], ALU.subtract)
+        ws_of_chunk = held.tile([P, GROUP, O], BF16, name="ws_of_chunk")
+        for q in range(GROUP):
+            row = q * QUAD
+            high_row = held.tile([P, O], BF16, name="high_row%d" % q)
+            nc.vector.tensor_scalar(high_row[:], ws_high[:], identity[:, row:row + 1], None, ALU.mult)
+            nc.vector.scalar_tensor_tensor(
+                ws_of_chunk[:, q, :], ws_low[:], identity[:, row + 1:row + 2], high_row[:],
+                ALU.mult, ALU.add,
+            )
+
+        operands = {}
+        outputs = {}
+        group_sums = {}
+        cosines = {}
+
+        def make_operands(c):
+            picked = offsets[:, c * W // 16:(c + 1) * W // 16]
+            xd_t = xd_tiles[c]
+            neg_xd = stream.tile([P, CB, W], F32, name="neg_xd")
+            nc.gpsimd.tensor_scalar(neg_xd[:], xd_t[:], -1.0, 0.0, ALU.mult, ALU.add)
+            d = stream.tile([P, CB, W], F32, name="d")
+            p = stream.tile([P, CB, W], F32, name="p")
+            for cb in range(CB):
+                nc.vector.tensor_tensor(
+                    d[:, cb, :], table[cb][:].indirect(picked), neg_xd[:, cb, :], ALU.add)
+            xs_bf = stream.tile([P, CB, W], BF16, name="xs_bf")
+            nc.vector.tensor_tensor(xs_bf[:], d[:], xd_t[:], ALU.add)
+            d_bf = stream.tile([P, CB, W], BF16, name="d_bf")
+            nc.vector.tensor_copy(d_bf[:], d[:])
+            for cb in range(CB):
+                nc.vector.tensor_tensor(
+                    p[:, cb, :], table[cb][:].indirect(picked), xd_t[:, cb, :], ALU.mult)
+            p_bf = stream.tile([P, CB, W], BF16, name="p_bf")
+            nc.vector.tensor_copy(p_bf[:], p[:])
+            xs_sq = stream.tile([P, CB, W], BF16, name="xs_sq")
+            nc.gpsimd.tensor_tensor(xs_sq[:], xs_bf[:], xs_bf[:], ALU.mult)
+            xd_sq = stream.tile([P, CB, W], BF16, name="xd_sq")
+            nc.gpsimd.tensor_tensor(xd_sq[:], xd_t[:], xd_t[:], ALU.mult)
+            operands[c] = {"xs": xs_bf, "d": d_bf, "p": p_bf, "xs_sq": xs_sq, "xd_sq": xd_sq}
+
+        def first_layers(c):
+            for name, wa_t, ba_t, wb_t, bb_t in branches:
+                h = operands[c][name]
+                u = hidden.tile([P, FB, W], BF16, name="u")
+                for fb in range(FB):
+                    acc = banks.tile([P, W], F32, name="acc")
+                    for cb in range(CB):
+                        nc.tensor.matmul(
+                            acc[:], wa_t[:, cb, fb * P:(fb + 1) * P], h[:, cb, :],
+                            start=cb == 0, stop=cb == CB - 1)
+                    nc.scalar.activation(u[:, fb, :], acc[:], ACT.Relu, bias=ba_t[:, fb:fb + 1])
+                operands[c]["u_" + name] = u
+
+        def column_sums(c):
+            q = c % GROUP
+            if q == 0:
+                for name in ("xs_sq", "xd_sq", "p"):
+                    group_sums[name] = sums.tile([P, W], F32, name="sum_" + name)
+            for name in ("xs_sq", "xd_sq", "p"):
+                for cb in range(CB):
+                    nc.tensor.matmul(
+                        group_sums[name][q * QUAD:(q + 1) * QUAD, :], ones[:], operands[c][name][:, cb, :],
+                        start=cb == 0, stop=cb == CB - 1)
+
+        def group_cosines(g):
+            norm_s = cosine.tile([P, W], F32, name="norm_s")
+            nc.scalar.activation(norm_s[:], group_sums["xs_sq"][:], ACT.Sqrt)
+            norm_d = cosine.tile([P, W], F32, name="norm_d")
+            nc.scalar.activation(norm_d[:], group_sums["xd_sq"][:], ACT.Sqrt)
+            dot = cosine.tile([P, W], F32, name="dot")
+            nc.scalar.copy(dot[:], group_sums["p"][:])
+            norms = cosine.tile([P, W], F32, name="norms")
+            nc.vector.tensor_tensor(norms[:], norm_s[:], norm_d[:], ALU.mult)
+            inverse = cosine.tile([P, W], F32, name="inverse")
+            nc.vector.reciprocal(inverse[:], norms[:])
+            cs_bf = cosine.tile([P, W], BF16, name="cs_bf")
+            nc.vector.tensor_tensor(cs_bf[:], dot[:], inverse[:], ALU.mult)
+            cosines[g] = cs_bf
+
+        def second_layers(c):
+            y = late.tile([P, len(branches), W], BF16, name="y")
+            for b, (name, wa_t, ba_t, wb_t, bb_t) in enumerate(branches):
+                u = operands[c]["u_" + name]
+                acc = banks.tile([P, W], F32, name="acc")
+                for fb in range(FB):
+                    nc.tensor.matmul(acc[:], wb_t[:, fb, :], u[:, fb, :],
+                                     start=fb == 0, stop=fb == FB - 1)
+                nc.scalar.activation(y[:, b, :], acc[:], ACT.Relu, bias=bb_t[:, 0:1])
+            outputs[c] = y
+
+        def final_layer(c):
+            y = outputs[c]
+            acc = banks.tile([P, W], F32, name="acc")
+            for b in range(len(branches)):
+                nc.tensor.matmul(acc[:], wf_t[:, b, :], y[:, b, :], start=b == 0, stop=False)
+            nc.tensor.matmul(acc[:], wf_t[:, ZB - 1, :], edge_t[:, c * W:(c + 1) * W],
+                             start=False, stop=False)
+            nc.tensor.matmul(acc[:], ws_of_chunk[:, c % GROUP, :], cosines[c // GROUP][:],
+                             start=False, stop=True)
+            out_t = stream.tile([P, W], F32, name="out_t")
+            nc.scalar.activation(out_t[:], acc[:], ACT.Tanh, bias=bfin_t[:, 0:1])
+            nc.scalar.dma_start(out[:, c * W:(c + 1) * W], out_t[:])
+
+        make_operands(0)
+        fetch_xd(2)
+        make_operands(1)
+        edge_t = load(nc.sync, [P, N], BF16, edge_attr, "edge_t")
+        for step in range(CHUNKS + FINAL_LAG):
+            if step + 3 < CHUNKS:
+                fetch_xd(step + 3)
+            if step + 2 < CHUNKS:
+                make_operands(step + 2)
+            if step < CHUNKS:
+                first_layers(step)
+                column_sums(step)
+                if step % GROUP == GROUP - 1:
+                    group_cosines(step // GROUP)
+            if 1 <= step <= CHUNKS:
+                second_layers(step - 1)
+            if step >= FINAL_LAG:
+                final_layer(step - FINAL_LAG)

@@ -108,7 +108,7 @@ def tile_edgeattrs_b_kernel(
             picked = offsets[:, c * W // 16:(c + 1) * W // 16]
             xd_t = xd_tiles[c]
             neg_xd = stream.tile([P, CB, W], F32, name="neg_xd")
-            nc.gpsimd.tensor_scalar(neg_xd[:], xd_t[:], -1.0, 0.0, ALU.mult, ALU.add)
+            nc.vector.tensor_scalar(neg_xd[:], xd_t[:], -1.0, None, ALU.mult)
             d = stream.tile([P, CB, W], F32, name="d")
             p = stream.tile([P, CB, W], F32, name="p")
             for cb in range(CB):
@@ -124,9 +124,9 @@ def tile_edgeattrs_b_kernel(
             p_bf = stream.tile([P, CB, W], BF16, name="p_bf")
             nc.vector.tensor_copy(p_bf[:], p[:])
             xs_sq = stream.tile([P, CB, W], BF16, name="xs_sq")
-            nc.gpsimd.tensor_tensor(xs_sq[:], xs_bf[:], xs_bf[:], ALU.mult)
+            nc.vector.tensor_tensor(xs_sq[:], xs_bf[:], xs_bf[:], ALU.mult)
             xd_sq = stream.tile([P, CB, W], BF16, name="xd_sq")
-            nc.gpsimd.tensor_tensor(xd_sq[:], xd_t[:], xd_t[:], ALU.mult)
+            nc.scalar.activation(xd_sq[:], xd_t[:], ACT.Square)
             operands[c] = {"xs": xs_bf, "d": d_bf, "p": p_bf, "xs_sq": xs_sq, "xd_sq": xd_sq}
 
         def first_layers(c):

@@ -78,8 +78,10 @@ def tile_edgeattrs_b_kernel(
         wf_t = load(nc.scalar, [P, ZB, O], BF16, wf.rearrange("(zb p) o -> p zb o", p=P), "wf_t")
         bfin_t = bias(bfin, 1, "bfin_t")
 
-        ones = held.tile([P, QUAD], BF16, name="ones")
-        nc.vector.memset(ones[:], 1.0)
+        quadrant_ones = held.tile([P, GROUP, P], BF16, name="quadrant_ones")
+        nc.vector.memset(quadrant_ones[:], 0.0)
+        for q in range(GROUP):
+            nc.vector.memset(quadrant_ones[:, q, q * QUAD:(q + 1) * QUAD], 1.0)
 
         identity = held.tile([P, P], F32, name="identity")
         make_identity(nc, identity[:])
@@ -102,13 +104,20 @@ def tile_edgeattrs_b_kernel(
         operands = {}
         outputs = {}
         group_sums = {}
+        inverses = {}
         cosines = {}
+        open_banks = {}
 
         def make_operands(c):
             picked = offsets[:, c * W // 16:(c + 1) * W // 16]
             xd_t = xd_tiles[c]
             neg_xd = stream.tile([P, CB, W], F32, name="neg_xd")
             nc.vector.tensor_scalar(neg_xd[:], xd_t[:], -1.0, None, ALU.mult)
+            xd_sq = stream.tile([P, CB, W], BF16, name="xd_sq")
+            if c % 2 == 0:
+                nc.vector.tensor_tensor(xd_sq[:], xd_t[:], xd_t[:], ALU.mult)
+            else:
+                nc.scalar.activation(xd_sq[:], xd_t[:], ACT.Square)
             d = stream.tile([P, CB, W], F32, name="d")
             p = stream.tile([P, CB, W], F32, name="p")
             for cb in range(CB):
@@ -116,6 +125,8 @@ def tile_edgeattrs_b_kernel(
                     d[:, cb, :], table[cb][:].indirect(picked), neg_xd[:, cb, :], ALU.add)
             xs_bf = stream.tile([P, CB, W], BF16, name="xs_bf")
             nc.vector.tensor_tensor(xs_bf[:], d[:], xd_t[:], ALU.add)
+            xs_sq = stream.tile([P, CB, W], BF16, name="xs_sq")
+            nc.vector.tensor_tensor(xs_sq[:], xs_bf[:], xs_bf[:], ALU.mult)
             d_bf = stream.tile([P, CB, W], BF16, name="d_bf")
             nc.vector.tensor_copy(d_bf[:], d[:])
             for cb in range(CB):
@@ -123,49 +134,44 @@ def tile_edgeattrs_b_kernel(
                     p[:, cb, :], table[cb][:].indirect(picked), xd_t[:, cb, :], ALU.mult)
             p_bf = stream.tile([P, CB, W], BF16, name="p_bf")
             nc.vector.tensor_copy(p_bf[:], p[:])
-            xs_sq = stream.tile([P, CB, W], BF16, name="xs_sq")
-            nc.vector.tensor_tensor(xs_sq[:], xs_bf[:], xs_bf[:], ALU.mult)
-            xd_sq = stream.tile([P, CB, W], BF16, name="xd_sq")
-            nc.scalar.activation(xd_sq[:], xd_t[:], ACT.Square)
             operands[c] = {"xs": xs_bf, "d": d_bf, "p": p_bf, "xs_sq": xs_sq, "xd_sq": xd_sq}
 
-        def first_layers(c):
-            for name, wa_t, ba_t, wb_t, bb_t in branches:
-                h = operands[c][name]
-                u = hidden.tile([P, FB, W], BF16, name="u")
-                for fb in range(FB):
-                    acc = banks.tile([P, W], F32, name="acc")
-                    for cb in range(CB):
-                        nc.tensor.matmul(
-                            acc[:], wa_t[:, cb, fb * P:(fb + 1) * P], h[:, cb, :],
-                            start=cb == 0, stop=cb == CB - 1)
-                    nc.scalar.activation(u[:, fb, :], acc[:], ACT.Relu, bias=ba_t[:, fb:fb + 1])
-                operands[c]["u_" + name] = u
-
-        def column_sums(c):
-            q = c % GROUP
-            if q == 0:
-                for name in ("xs_sq", "xd_sq", "p"):
-                    group_sums[name] = sums.tile([P, W], F32, name="sum_" + name)
-            for name in ("xs_sq", "xd_sq", "p"):
+        def first_layer(c, branch):
+            name, wa_t, ba_t, wb_t, bb_t = branch
+            h = operands[c][name]
+            u = hidden.tile([P, FB, W], BF16, name="u")
+            for fb in range(FB):
+                acc = banks.tile([P, W], F32, name="acc")
                 for cb in range(CB):
                     nc.tensor.matmul(
-                        group_sums[name][q * QUAD:(q + 1) * QUAD, :], ones[:], operands[c][name][:, cb, :],
+                        acc[:], wa_t[:, cb, fb * P:(fb + 1) * P], h[:, cb, :],
                         start=cb == 0, stop=cb == CB - 1)
+                nc.scalar.activation(u[:, fb, :], acc[:], ACT.Relu, bias=ba_t[:, fb:fb + 1])
+            operands[c]["u_" + name] = u
+
+        def column_sum(c, name):
+            q = c % GROUP
+            if q == 0:
+                group_sums[name] = sums.tile([P, W], F32, name="sum_" + name)
+            for cb in range(CB):
+                nc.tensor.matmul(
+                    group_sums[name][:], quadrant_ones[:, q, :], operands[c][name][:, cb, :],
+                    start=q == 0 and cb == 0, stop=q == GROUP - 1 and cb == CB - 1)
+
+        def inverse_norms(g):
+            inv_s = cosine.tile([P, W], F32, name="inv_s")
+            nc.scalar.activation(inv_s[:], group_sums["xs_sq"][:], ACT.Abs_reciprocal_sqrt)
+            inv_d = cosine.tile([P, W], F32, name="inv_d")
+            nc.scalar.activation(inv_d[:], group_sums["xd_sq"][:], ACT.Abs_reciprocal_sqrt)
+            inverse = cosine.tile([P, W], F32, name="inverse")
+            nc.gpsimd.tensor_tensor(inverse[:], inv_s[:], inv_d[:], ALU.mult)
+            inverses[g] = inverse
 
         def group_cosines(g):
-            norm_s = cosine.tile([P, W], F32, name="norm_s")
-            nc.scalar.activation(norm_s[:], group_sums["xs_sq"][:], ACT.Sqrt)
-            norm_d = cosine.tile([P, W], F32, name="norm_d")
-            nc.scalar.activation(norm_d[:], group_sums["xd_sq"][:], ACT.Sqrt)
             dot = cosine.tile([P, W], F32, name="dot")
             nc.scalar.copy(dot[:], group_sums["p"][:])
-            norms = cosine.tile([P, W], F32, name="norms")
-            nc.vector.tensor_tensor(norms[:], norm_s[:], norm_d[:], ALU.mult)
-            inverse = cosine.tile([P, W], F32, name="inverse")
-            nc.vector.reciprocal(inverse[:], norms[:])
             cs_bf = cosine.tile([P, W], BF16, name="cs_bf")
-            nc.vector.tensor_tensor(cs_bf[:], dot[:], inverse[:], ALU.mult)
+            nc.gpsimd.tensor_tensor(cs_bf[:], dot[:], inverses[g][:], ALU.mult)
             cosines[g] = cs_bf
 
         def second_layers(c):
@@ -179,34 +185,50 @@ def tile_edgeattrs_b_kernel(
                 nc.scalar.activation(y[:, b, :], acc[:], ACT.Relu, bias=bb_t[:, 0:1])
             outputs[c] = y
 
-        def final_layer(c):
+        def open_final(c):
             y = outputs[c]
             acc = banks.tile([P, W], F32, name="acc")
             for b in range(len(branches)):
                 nc.tensor.matmul(acc[:], wf_t[:, b, :], y[:, b, :], start=b == 0, stop=False)
             nc.tensor.matmul(acc[:], wf_t[:, ZB - 1, :], edge_t[:, c * W:(c + 1) * W],
                              start=False, stop=False)
+            open_banks[c] = acc
+
+        def close_final(c):
+            acc = open_banks[c]
             nc.tensor.matmul(acc[:], ws_of_chunk[:, c % GROUP, :], cosines[c // GROUP][:],
                              start=False, stop=True)
             out_t = stream.tile([P, W], F32, name="out_t")
             nc.scalar.activation(out_t[:], acc[:], ACT.Tanh, bias=bfin_t[:, 0:1])
-            nc.scalar.dma_start(out[:, c * W:(c + 1) * W], out_t[:])
+            nc.sync.dma_start(out[:, c * W:(c + 1) * W], out_t[:])
 
         make_operands(0)
         fetch_xd(2)
         make_operands(1)
         edge_t = load(nc.sync, [P, N], BF16, edge_attr, "edge_t")
-        for step in range(CHUNKS + FINAL_LAG):
+        for step in range(CHUNKS):
             if step + 3 < CHUNKS:
                 fetch_xd(step + 3)
             if step + 2 < CHUNKS:
                 make_operands(step + 2)
-            if step < CHUNKS:
-                first_layers(step)
-                column_sums(step)
-                if step % GROUP == GROUP - 1:
-                    group_cosines(step // GROUP)
-            if 1 <= step <= CHUNKS:
+            last_of_group = step % GROUP == GROUP - 1
+            first_layer(step, branches[0])
+            first_layer(step, branches[1])
+            column_sum(step, "xs_sq")
+            column_sum(step, "xd_sq")
+            if last_of_group:
+                inverse_norms(step // GROUP)
+            if step >= 1:
                 second_layers(step - 1)
             if step >= FINAL_LAG:
-                final_layer(step - FINAL_LAG)
+                open_final(step - FINAL_LAG)
+                close_final(step - FINAL_LAG)
+            column_sum(step, "p")
+            if last_of_group:
+                group_cosines(step // GROUP)
+            first_layer(step, branches[2])
+        second_layers(CHUNKS - 1)
+        for c in range(CHUNKS - FINAL_LAG, CHUNKS):
+            open_final(c)
+        for c in range(CHUNKS - FINAL_LAG, CHUNKS):
+            close_final(c)

@@ -16,7 +16,7 @@ W = 512
 CHUNKS = N // W
 GROUP = 4
 QUAD = P // GROUP
-FINAL_LAG = GROUP
+FINAL_LAG = GROUP + 2
 
 FLOPS = 2 * N * (3 * C * F + 3 * F * O + Z * O)
 
@@ -114,10 +114,7 @@ def tile_edgeattrs_b_kernel(
             neg_xd = stream.tile([P, CB, W], F32, name="neg_xd")
             nc.vector.tensor_scalar(neg_xd[:], xd_t[:], -1.0, None, ALU.mult)
             xd_sq = stream.tile([P, CB, W], BF16, name="xd_sq")
-            if c % 2 == 0:
-                nc.vector.tensor_tensor(xd_sq[:], xd_t[:], xd_t[:], ALU.mult)
-            else:
-                nc.scalar.activation(xd_sq[:], xd_t[:], ACT.Square)
+            nc.scalar.activation(xd_sq[:], xd_t[:], ACT.Square)
             d = stream.tile([P, CB, W], F32, name="d")
             p = stream.tile([P, CB, W], F32, name="p")
             for cb in range(CB):
@@ -164,14 +161,14 @@ def tile_edgeattrs_b_kernel(
             inv_d = cosine.tile([P, W], F32, name="inv_d")
             nc.scalar.activation(inv_d[:], group_sums["xd_sq"][:], ACT.Abs_reciprocal_sqrt)
             inverse = cosine.tile([P, W], F32, name="inverse")
-            nc.gpsimd.tensor_tensor(inverse[:], inv_s[:], inv_d[:], ALU.mult)
+            nc.vector.tensor_tensor(inverse[:], inv_s[:], inv_d[:], ALU.mult)
             inverses[g] = inverse
 
         def group_cosines(g):
             dot = cosine.tile([P, W], F32, name="dot")
             nc.scalar.copy(dot[:], group_sums["p"][:])
             cs_bf = cosine.tile([P, W], BF16, name="cs_bf")
-            nc.gpsimd.tensor_tensor(cs_bf[:], dot[:], inverses[g][:], ALU.mult)
+            nc.vector.tensor_tensor(cs_bf[:], dot[:], inverses[g][:], ALU.mult)
             cosines[g] = cs_bf
 
         def second_layers(c):
@@ -228,7 +225,10 @@ def tile_edgeattrs_b_kernel(
                 group_cosines(step // GROUP)
             first_layer(step, branches[2])
         second_layers(CHUNKS - 1)
-        for c in range(CHUNKS - FINAL_LAG, CHUNKS):
+        for c in range(CHUNKS - FINAL_LAG, CHUNKS - GROUP):
             open_final(c)
-        for c in range(CHUNKS - FINAL_LAG, CHUNKS):
+            close_final(c)
+        for c in range(CHUNKS - GROUP, CHUNKS):
+            open_final(c)
+        for c in range(CHUNKS - GROUP, CHUNKS):
             close_final(c)

@@ -33,8 +33,7 @@ def tile_edgeattrs_b_kernel(
         tc.tile_pool(name="hidden", bufs=6) as hidden,
         tc.tile_pool(name="late", bufs=FINAL_LAG + 2) as late,
         tc.tile_pool(name="cosine", bufs=2) as cosine,
-        tc.psum_pool(name="sums", bufs=1) as sums,
-        tc.psum_pool(name="banks", bufs=5) as banks,
+        tc.psum_pool(name="banks", bufs=8) as banks,
     ):
         def load(queue, shape, dtype, source, name):
             tile = held.tile(shape, dtype, name=name)
@@ -59,10 +58,10 @@ def tile_edgeattrs_b_kernel(
         fetch_xd(1)
 
         def first_weight(w, name):
-            return load(nc.scalar, [P, CB, F], BF16, w.rearrange("(cb p) f -> p cb f", p=P), name)
+            return load(nc.sync, [P, CB, F], BF16, w.rearrange("(cb p) f -> p cb f", p=P), name)
 
         def second_weight(w, name):
-            return load(nc.scalar, [P, FB, O], BF16, w.rearrange("(fb p) o -> p fb o", p=P), name)
+            return load(nc.sync, [P, FB, O], BF16, w.rearrange("(fb p) o -> p fb o", p=P), name)
 
         def bias(b, blocks, name):
             return load(nc.scalar, [P, blocks], F32, b.rearrange("(a p) o -> p (a o)", p=P), name)
@@ -75,13 +74,11 @@ def tile_edgeattrs_b_kernel(
             ("p", first_weight(w4a, "w4a_t"), bias(b4a, FB, "b4a_t"),
              second_weight(w4b, "w4b_t"), bias(b4b, 1, "b4b_t")),
         )
-        wf_t = load(nc.scalar, [P, ZB, O], BF16, wf.rearrange("(zb p) o -> p zb o", p=P), "wf_t")
+        wf_t = load(nc.sync, [P, ZB, O], BF16, wf.rearrange("(zb p) o -> p zb o", p=P), "wf_t")
         bfin_t = bias(bfin, 1, "bfin_t")
 
-        quadrant_ones = held.tile([P, GROUP, P], BF16, name="quadrant_ones")
-        nc.vector.memset(quadrant_ones[:], 0.0)
-        for q in range(GROUP):
-            nc.vector.memset(quadrant_ones[:, q, q * QUAD:(q + 1) * QUAD], 1.0)
+        ones = held.tile([P, QUAD], BF16, name="ones")
+        nc.vector.memset(ones[:], 1.0)
 
         identity = held.tile([P, P], F32, name="identity")
         make_identity(nc, identity[:])
@@ -103,8 +100,6 @@ def tile_edgeattrs_b_kernel(
 
         operands = {}
         outputs = {}
-        group_sums = {}
-        inverses = {}
         cosines = {}
         open_banks = {}
 
@@ -113,7 +108,7 @@ def tile_edgeattrs_b_kernel(
             xd_t = xd_tiles[c]
             neg_xd = stream.tile([P, CB, W], F32, name="neg_xd")
             nc.vector.tensor_scalar(neg_xd[:], xd_t[:], -1.0, None, ALU.mult)
-            xd_sq = stream.tile([P, CB, W], BF16, name="xd_sq")
+            xd_sq = stream.tile([P, CB, W], BF16, name="xd_sq", bufs=GROUP + 3)
             nc.scalar.activation(xd_sq[:], xd_t[:], ACT.Square)
             d = stream.tile([P, CB, W], F32, name="d")
             p = stream.tile([P, CB, W], F32, name="p")
@@ -122,14 +117,14 @@ def tile_edgeattrs_b_kernel(
                     d[:, cb, :], table[cb][:].indirect(picked), neg_xd[:, cb, :], ALU.add)
             xs_bf = stream.tile([P, CB, W], BF16, name="xs_bf")
             nc.vector.tensor_tensor(xs_bf[:], d[:], xd_t[:], ALU.add)
-            xs_sq = stream.tile([P, CB, W], BF16, name="xs_sq")
+            xs_sq = stream.tile([P, CB, W], BF16, name="xs_sq", bufs=GROUP + 3)
             nc.vector.tensor_tensor(xs_sq[:], xs_bf[:], xs_bf[:], ALU.mult)
             d_bf = stream.tile([P, CB, W], BF16, name="d_bf")
             nc.vector.tensor_copy(d_bf[:], d[:])
             for cb in range(CB):
                 nc.vector.tensor_tensor(
                     p[:, cb, :], table[cb][:].indirect(picked), xd_t[:, cb, :], ALU.mult)
-            p_bf = stream.tile([P, CB, W], BF16, name="p_bf")
+            p_bf = stream.tile([P, CB, W], BF16, name="p_bf", bufs=GROUP + 3)
             nc.vector.tensor_copy(p_bf[:], p[:])
             operands[c] = {"xs": xs_bf, "d": d_bf, "p": p_bf, "xs_sq": xs_sq, "xd_sq": xd_sq}
 
@@ -146,29 +141,26 @@ def tile_edgeattrs_b_kernel(
                 nc.scalar.activation(u[:, fb, :], acc[:], ACT.Relu, bias=ba_t[:, fb:fb + 1])
             operands[c]["u_" + name] = u
 
-        def column_sum(c, name):
-            q = c % GROUP
-            if q == 0:
-                group_sums[name] = sums.tile([P, W], F32, name="sum_" + name)
-            for cb in range(CB):
-                nc.tensor.matmul(
-                    group_sums[name][:], quadrant_ones[:, q, :], operands[c][name][:, cb, :],
-                    start=q == 0 and cb == 0, stop=q == GROUP - 1 and cb == CB - 1)
-
-        def inverse_norms(g):
+        def group_cosines(g):
+            group_sums = {}
+            for name in ("xs_sq", "xd_sq", "p"):
+                group_sums[name] = banks.tile([P, W], F32, name="acc")
+                for q in range(GROUP):
+                    for cb in range(CB):
+                        nc.tensor.matmul(
+                            group_sums[name][q * QUAD:(q + 1) * QUAD, :], ones[:],
+                            operands[g * GROUP + q][name][:, cb, :],
+                            start=cb == 0, stop=cb == CB - 1)
             inv_s = cosine.tile([P, W], F32, name="inv_s")
             nc.scalar.activation(inv_s[:], group_sums["xs_sq"][:], ACT.Abs_reciprocal_sqrt)
             inv_d = cosine.tile([P, W], F32, name="inv_d")
             nc.scalar.activation(inv_d[:], group_sums["xd_sq"][:], ACT.Abs_reciprocal_sqrt)
-            inverse = cosine.tile([P, W], F32, name="inverse")
-            nc.vector.tensor_tensor(inverse[:], inv_s[:], inv_d[:], ALU.mult)
-            inverses[g] = inverse
-
-        def group_cosines(g):
             dot = cosine.tile([P, W], F32, name="dot")
             nc.scalar.copy(dot[:], group_sums["p"][:])
+            inverse = cosine.tile([P, W], F32, name="inverse")
+            nc.vector.tensor_tensor(inverse[:], inv_s[:], inv_d[:], ALU.mult)
             cs_bf = cosine.tile([P, W], BF16, name="cs_bf")
-            nc.vector.tensor_tensor(cs_bf[:], dot[:], inverses[g][:], ALU.mult)
+            nc.vector.tensor_tensor(cs_bf[:], dot[:], inverse[:], ALU.mult)
             cosines[g] = cs_bf
 
         def second_layers(c):
@@ -208,22 +200,16 @@ def tile_edgeattrs_b_kernel(
                 fetch_xd(step + 3)
             if step + 2 < CHUNKS:
                 make_operands(step + 2)
-            last_of_group = step % GROUP == GROUP - 1
             first_layer(step, branches[0])
             first_layer(step, branches[1])
-            column_sum(step, "xs_sq")
-            column_sum(step, "xd_sq")
-            if last_of_group:
-                inverse_norms(step // GROUP)
             if step >= 1:
                 second_layers(step - 1)
             if step >= FINAL_LAG:
                 open_final(step - FINAL_LAG)
                 close_final(step - FINAL_LAG)
-            column_sum(step, "p")
-            if last_of_group:
-                group_cosines(step // GROUP)
             first_layer(step, branches[2])
+            if step % GROUP == GROUP - 1:
+                group_cosines(step // GROUP)
         second_layers(CHUNKS - 1)
         for c in range(CHUNKS - FINAL_LAG, CHUNKS - GROUP):
             open_final(c)

@@ -16,6 +16,7 @@ W = 512
 CHUNKS = N // W
 GROUP = 4
 QUAD = P // GROUP
+TABLE_PIECES = 4
 FINAL_LAG = GROUP + 2
 
 FLOPS = 2 * N * (3 * C * F + 3 * F * O + Z * O)
@@ -51,10 +52,11 @@ def tile_edgeattrs_b_kernel(
             xd_tiles[c] = xd_t
 
         fetch_xd(0)
-        table = [
-            load(nc.sync, [P, S], F32, x[cb * P:(cb + 1) * P, :], "table%d" % cb)
-            for cb in range(CB)
-        ]
+        table = [held.tile([P, S], F32, name="table%d" % cb) for cb in range(CB)]
+        for cb in range(CB):
+            for k in range(TABLE_PIECES):
+                columns = slice(k * S // TABLE_PIECES, (k + 1) * S // TABLE_PIECES)
+                nc.sync.dma_start(table[cb][:, columns], x[cb * P:(cb + 1) * P, columns])
         fetch_xd(1)
 
         def first_weight(w, name):
@@ -107,25 +109,27 @@ def tile_edgeattrs_b_kernel(
             picked = offsets[:, c * W // 16:(c + 1) * W // 16]
             xd_t = xd_tiles[c]
             neg_xd = stream.tile([P, CB, W], F32, name="neg_xd")
-            nc.vector.tensor_scalar(neg_xd[:], xd_t[:], -1.0, None, ALU.mult)
             xd_sq = stream.tile([P, CB, W], BF16, name="xd_sq", bufs=GROUP + 3)
-            nc.scalar.activation(xd_sq[:], xd_t[:], ACT.Square)
             d = stream.tile([P, CB, W], F32, name="d")
             p = stream.tile([P, CB, W], F32, name="p")
-            for cb in range(CB):
-                nc.vector.tensor_tensor(
-                    d[:, cb, :], table[cb][:].indirect(picked), neg_xd[:, cb, :], ALU.add)
             xs_bf = stream.tile([P, CB, W], BF16, name="xs_bf")
-            nc.vector.tensor_tensor(xs_bf[:], d[:], xd_t[:], ALU.add)
             xs_sq = stream.tile([P, CB, W], BF16, name="xs_sq", bufs=GROUP + 3)
-            nc.vector.tensor_tensor(xs_sq[:], xs_bf[:], xs_bf[:], ALU.mult)
             d_bf = stream.tile([P, CB, W], BF16, name="d_bf")
-            nc.vector.tensor_copy(d_bf[:], d[:])
-            for cb in range(CB):
-                nc.vector.tensor_tensor(
-                    p[:, cb, :], table[cb][:].indirect(picked), xd_t[:, cb, :], ALU.mult)
             p_bf = stream.tile([P, CB, W], BF16, name="p_bf", bufs=GROUP + 3)
-            nc.vector.tensor_copy(p_bf[:], p[:])
+            spans = [slice(cb, cb + 1) for cb in range(CB)] if c == 0 else [slice(0, CB)]
+            for span in spans:
+                nc.vector.tensor_scalar(neg_xd[:, span, :], xd_t[:, span, :], -1.0, None, ALU.mult)
+                nc.scalar.activation(xd_sq[:, span, :], xd_t[:, span, :], ACT.Square)
+                for cb in range(span.start, span.stop):
+                    nc.vector.tensor_tensor(
+                        d[:, cb, :], table[cb][:].indirect(picked), neg_xd[:, cb, :], ALU.add)
+                nc.vector.tensor_tensor(xs_bf[:, span, :], d[:, span, :], xd_t[:, span, :], ALU.add)
+                nc.vector.tensor_tensor(xs_sq[:, span, :], xs_bf[:, span, :], xs_bf[:, span, :], ALU.mult)
+                nc.vector.tensor_copy(d_bf[:, span, :], d[:, span, :])
+                for cb in range(span.start, span.stop):
+                    nc.vector.tensor_tensor(
+                        p[:, cb, :], table[cb][:].indirect(picked), xd_t[:, cb, :], ALU.mult)
+                nc.vector.tensor_copy(p_bf[:, span, :], p[:, span, :])
             operands[c] = {"xs": xs_bf, "d": d_bf, "p": p_bf, "xs_sq": xs_sq, "xd_sq": xd_sq}
 
         def first_layer(c, branch):
@@ -187,7 +191,7 @@ def tile_edgeattrs_b_kernel(
             acc = open_banks[c]
             nc.tensor.matmul(acc[:], ws_of_chunk[:, c % GROUP, :], cosines[c // GROUP][:],
                              start=False, stop=True)
-            out_t = stream.tile([P, W], F32, name="out_t")
+            out_t = stream.tile([P, W], F32, name="out_t", bufs=GROUP + 2)
             nc.scalar.activation(out_t[:], acc[:], ACT.Tanh, bias=bfin_t[:, 0:1])
             nc.sync.dma_start(out[:, c * W:(c + 1) * W], out_t[:])
 

@@ -16,7 +16,7 @@ W = 512
 CHUNKS = N // W
 GROUP = 4
 QUAD = P // GROUP
-TABLE_PIECES = 4
+TABLE_PIECES = 8
 FINAL_LAG = GROUP + 2
 
 FLOPS = 2 * N * (3 * C * F + 3 * F * O + Z * O)
@@ -102,6 +102,7 @@ def tile_edgeattrs_b_kernel(
 
         operands = {}
         outputs = {}
+        inverses = {}
         cosines = {}
         open_banks = {}
 
@@ -132,7 +133,13 @@ def tile_edgeattrs_b_kernel(
                 nc.vector.tensor_copy(p_bf[:, span, :], p[:, span, :])
             operands[c] = {"xs": xs_bf, "d": d_bf, "p": p_bf, "xs_sq": xs_sq, "xd_sq": xd_sq}
 
-        def first_layer(c, branch):
+        def relu(out_ap, acc, bias_column, by_vector):
+            if by_vector:
+                nc.vector.tensor_scalar(out_ap, acc[:], bias_column, 0.0, ALU.add, ALU.max)
+            else:
+                nc.scalar.activation(out_ap, acc[:], ACT.Relu, bias=bias_column)
+
+        def first_layer(c, branch, by_vector=False):
             name, wa_t, ba_t, wb_t, bb_t = branch
             h = operands[c][name]
             u = hidden.tile([P, FB, W], BF16, name="u")
@@ -142,41 +149,50 @@ def tile_edgeattrs_b_kernel(
                     nc.tensor.matmul(
                         acc[:], wa_t[:, cb, fb * P:(fb + 1) * P], h[:, cb, :],
                         start=cb == 0, stop=cb == CB - 1)
-                nc.scalar.activation(u[:, fb, :], acc[:], ACT.Relu, bias=ba_t[:, fb:fb + 1])
+                relu(u[:, fb, :], acc, ba_t[:, fb:fb + 1], by_vector)
             operands[c]["u_" + name] = u
 
-        def group_cosines(g):
-            group_sums = {}
-            for name in ("xs_sq", "xd_sq", "p"):
-                group_sums[name] = banks.tile([P, W], F32, name="acc")
-                for q in range(GROUP):
-                    for cb in range(CB):
-                        nc.tensor.matmul(
-                            group_sums[name][q * QUAD:(q + 1) * QUAD, :], ones[:],
-                            operands[g * GROUP + q][name][:, cb, :],
-                            start=cb == 0, stop=cb == CB - 1)
+        def group_sums(g, name):
+            sums = banks.tile([P, W], F32, name="acc")
+            for q in range(GROUP):
+                for cb in range(CB):
+                    nc.tensor.matmul(
+                        sums[q * QUAD:(q + 1) * QUAD, :], ones[:],
+                        operands[g * GROUP + q][name][:, cb, :],
+                        start=cb == 0, stop=cb == CB - 1)
+            return sums
+
+        def group_norms(g):
+            sums_s = group_sums(g, "xs_sq")
+            sums_d = group_sums(g, "xd_sq")
             inv_s = cosine.tile([P, W], F32, name="inv_s")
-            nc.scalar.activation(inv_s[:], group_sums["xs_sq"][:], ACT.Abs_reciprocal_sqrt)
+            nc.scalar.activation(inv_s[:], sums_s[:], ACT.Abs_reciprocal_sqrt)
             inv_d = cosine.tile([P, W], F32, name="inv_d")
-            nc.scalar.activation(inv_d[:], group_sums["xd_sq"][:], ACT.Abs_reciprocal_sqrt)
-            dot = cosine.tile([P, W], F32, name="dot")
-            nc.scalar.copy(dot[:], group_sums["p"][:])
+            nc.scalar.activation(inv_d[:], sums_d[:], ACT.Abs_reciprocal_sqrt)
             inverse = cosine.tile([P, W], F32, name="inverse")
             nc.vector.tensor_tensor(inverse[:], inv_s[:], inv_d[:], ALU.mult)
+            inverses[g] = inverse
+
+        def group_cosines(g, vector_is_free):
+            dot = group_sums(g, "p")
+            if not vector_is_free:
+                dot_copy = cosine.tile([P, W], F32, name="dot_copy")
+                nc.scalar.copy(dot_copy[:], dot[:])
+                dot = dot_copy
             cs_bf = cosine.tile([P, W], BF16, name="cs_bf")
-            nc.vector.tensor_tensor(cs_bf[:], dot[:], inverse[:], ALU.mult)
+            nc.vector.tensor_tensor(cs_bf[:], dot[:], inverses[g][:], ALU.mult)
             cosines[g] = cs_bf
 
-        def second_layers(c):
-            y = late.tile([P, len(branches), W], BF16, name="y")
-            for b, (name, wa_t, ba_t, wb_t, bb_t) in enumerate(branches):
-                u = operands[c]["u_" + name]
-                acc = banks.tile([P, W], F32, name="acc")
-                for fb in range(FB):
-                    nc.tensor.matmul(acc[:], wb_t[:, fb, :], u[:, fb, :],
-                                     start=fb == 0, stop=fb == FB - 1)
-                nc.scalar.activation(y[:, b, :], acc[:], ACT.Relu, bias=bb_t[:, 0:1])
-            outputs[c] = y
+        def second_layer(c, b, by_vector=False):
+            name, wa_t, ba_t, wb_t, bb_t = branches[b]
+            if b == 0:
+                outputs[c] = late.tile([P, len(branches), W], BF16, name="y")
+            u = operands[c]["u_" + name]
+            acc = banks.tile([P, W], F32, name="acc")
+            for fb in range(FB):
+                nc.tensor.matmul(acc[:], wb_t[:, fb, :], u[:, fb, :],
+                                 start=fb == 0, stop=fb == FB - 1)
+            relu(outputs[c][:, b, :], acc, bb_t[:, 0:1], by_vector)
 
         def open_final(c):
             y = outputs[c]
@@ -204,21 +220,30 @@ def tile_edgeattrs_b_kernel(
                 fetch_xd(step + 3)
             if step + 2 < CHUNKS:
                 make_operands(step + 2)
+            last_step = step == CHUNKS - 1
+            if step - 2 >= CHUNKS - GROUP:
+                open_final(step - 2)
             first_layer(step, branches[0])
+            if last_step:
+                group_norms(step // GROUP)
             first_layer(step, branches[1])
             if step >= 1:
-                second_layers(step - 1)
+                second_layer(step - 1, 2)
             if step >= FINAL_LAG:
                 open_final(step - FINAL_LAG)
                 close_final(step - FINAL_LAG)
-            first_layer(step, branches[2])
+            first_layer(step, branches[2], by_vector=last_step)
+            second_layer(step, 0, by_vector=last_step)
+            second_layer(step, 1, by_vector=last_step)
             if step % GROUP == GROUP - 1:
-                group_cosines(step // GROUP)
-        second_layers(CHUNKS - 1)
+                if not last_step:
+                    group_norms(step // GROUP)
+                group_cosines(step // GROUP, vector_is_free=last_step)
+        second_layer(CHUNKS - 1, 2, by_vector=True)
         for c in range(CHUNKS - FINAL_LAG, CHUNKS - GROUP):
             open_final(c)
             close_final(c)
-        for c in range(CHUNKS - GROUP, CHUNKS):
+        for c in range(CHUNKS - 2, CHUNKS):
             open_final(c)
         for c in range(CHUNKS - GROUP, CHUNKS):
             close_final(c)

@@ -16,7 +16,7 @@ W = 512
 CHUNKS = N // W
 GROUP = 4
 QUAD = P // GROUP
-TABLE_PIECES = 8
+TABLE_PIECES = 4
 FINAL_LAG = GROUP + 2
 
 FLOPS = 2 * N * (3 * C * F + 3 * F * O + Z * O)
@@ -120,7 +120,10 @@ def tile_edgeattrs_b_kernel(
             spans = [slice(cb, cb + 1) for cb in range(CB)] if c == 0 else [slice(0, CB)]
             for span in spans:
                 nc.vector.tensor_scalar(neg_xd[:, span, :], xd_t[:, span, :], -1.0, None, ALU.mult)
-                nc.scalar.activation(xd_sq[:, span, :], xd_t[:, span, :], ACT.Square)
+                if c % GROUP == (GROUP - 1 + 2) % GROUP:
+                    nc.vector.tensor_tensor(xd_sq[:, span, :], xd_t[:, span, :], xd_t[:, span, :], ALU.mult)
+                else:
+                    nc.scalar.activation(xd_sq[:, span, :], xd_t[:, span, :], ACT.Square)
                 for cb in range(span.start, span.stop):
                     nc.vector.tensor_tensor(
                         d[:, cb, :], table[cb][:].indirect(picked), neg_xd[:, cb, :], ALU.add)

@@ -200,10 +200,10 @@ def tile_edgeattrs_b_kernel(
         def open_final(c):
             y = outputs[c]
             acc = banks.tile([P, W], F32, name="acc")
-            for b in range(len(branches)):
-                nc.tensor.matmul(acc[:], wf_t[:, b, :], y[:, b, :], start=b == 0, stop=False)
             nc.tensor.matmul(acc[:], wf_t[:, ZB - 1, :], edge_t[:, c * W:(c + 1) * W],
-                             start=False, stop=False)
+                             start=True, stop=False)
+            for b in range(len(branches)):
+                nc.tensor.matmul(acc[:], wf_t[:, b, :], y[:, b, :], start=False, stop=False)
             open_banks[c] = acc
 
         def close_final(c):
@@ -218,35 +218,39 @@ def tile_edgeattrs_b_kernel(
         fetch_xd(2)
         make_operands(1)
         edge_t = load(nc.sync, [P, N], BF16, edge_attr, "edge_t")
-        for step in range(CHUNKS):
+        for step in range(CHUNKS - 1):
             if step + 3 < CHUNKS:
                 fetch_xd(step + 3)
             if step + 2 < CHUNKS:
                 make_operands(step + 2)
-            last_step = step == CHUNKS - 1
             if step - 2 >= CHUNKS - GROUP:
                 open_final(step - 2)
             first_layer(step, branches[0])
-            if last_step:
-                group_norms(step // GROUP)
             first_layer(step, branches[1])
             if step >= 1:
                 second_layer(step - 1, 2)
             if step >= FINAL_LAG:
                 open_final(step - FINAL_LAG)
                 close_final(step - FINAL_LAG)
-            first_layer(step, branches[2], by_vector=last_step)
-            second_layer(step, 0, by_vector=last_step)
-            second_layer(step, 1, by_vector=last_step)
+            first_layer(step, branches[2])
+            second_layer(step, 0)
+            second_layer(step, 1)
             if step % GROUP == GROUP - 1:
-                if not last_step:
-                    group_norms(step // GROUP)
-                group_cosines(step // GROUP, vector_is_free=last_step)
-        second_layer(CHUNKS - 1, 2, by_vector=True)
-        for c in range(CHUNKS - FINAL_LAG, CHUNKS - GROUP):
+                group_norms(step // GROUP)
+                group_cosines(step // GROUP, vector_is_free=False)
+        last = CHUNKS - 1
+        first_layer(last, branches[0])
+        first_layer(last, branches[1])
+        group_norms(last // GROUP)
+        first_layer(last, branches[2], by_vector=True)
+        group_cosines(last // GROUP, vector_is_free=True)
+        for b in range(len(branches)):
+            second_layer(last, b, by_vector=True)
+        second_layer(last - 1, 2)
+        for c in range(last - FINAL_LAG, CHUNKS - GROUP):
             open_final(c)
             close_final(c)
-        for c in range(CHUNKS - 2, CHUNKS):
+        for c in range(last - 2, CHUNKS):
             open_final(c)
         for c in range(CHUNKS - GROUP, CHUNKS):
             close_final(c)

@@ -17,7 +17,7 @@ CHUNKS = N // W
 GROUP = 4
 QUAD = P // GROUP
 TABLE_PIECES = 4
-FINAL_LAG = GROUP + 2
+FINAL_LAG = GROUP + 1
 
 FLOPS = 2 * N * (3 * C * F + 3 * F * O + Z * O)
 
@@ -223,6 +223,9 @@ def tile_edgeattrs_b_kernel(
                 fetch_xd(step + 3)
             if step + 2 < CHUNKS:
                 make_operands(step + 2)
+            if step % GROUP == GROUP - 1:
+                group_norms(step // GROUP)
+                group_cosines(step // GROUP, vector_is_free=False)
             if step - 2 >= CHUNKS - GROUP:
                 open_final(step - 2)
             first_layer(step, branches[0])
@@ -235,12 +238,9 @@ def tile_edgeattrs_b_kernel(
             first_layer(step, branches[2])
             second_layer(step, 0)
             second_layer(step, 1)
-            if step % GROUP == GROUP - 1:
-                group_norms(step // GROUP)
-                group_cosines(step // GROUP, vector_is_free=False)
         last = CHUNKS - 1
-        first_layer(last, branches[0])
-        first_layer(last, branches[1])
+        first_layer(last, branches[0], by_vector=True)
+        first_layer(last, branches[1], by_vector=True)
         group_norms(last // GROUP)
         first_layer(last, branches[2], by_vector=True)
         group_cosines(last // GROUP, vector_is_free=True)

@@ -106,35 +106,50 @@ def tile_edgeattrs_b_kernel(
         cosines = {}
         open_banks = {}
 
-        def make_operands(c):
+        def spans_of(c):
+            return [slice(cb, cb + 1) for cb in range(CB)] if c == 0 else [slice(0, CB)]
+
+        def picked_tile(name):
+            return stream.tile([P, CB, W], F32, name=name, tag="picked", bufs=2)
+
+        def make_difference(c, span):
             picked = offsets[:, c * W // 16:(c + 1) * W // 16]
             xd_t = xd_tiles[c]
-            neg_xd = stream.tile([P, CB, W], F32, name="neg_xd")
-            xd_sq = stream.tile([P, CB, W], BF16, name="xd_sq", bufs=GROUP + 3)
-            d = stream.tile([P, CB, W], F32, name="d")
-            p = stream.tile([P, CB, W], F32, name="p")
-            xs_bf = stream.tile([P, CB, W], BF16, name="xs_bf")
-            xs_sq = stream.tile([P, CB, W], BF16, name="xs_sq", bufs=GROUP + 3)
-            d_bf = stream.tile([P, CB, W], BF16, name="d_bf")
-            p_bf = stream.tile([P, CB, W], BF16, name="p_bf", bufs=GROUP + 3)
-            spans = [slice(cb, cb + 1) for cb in range(CB)] if c == 0 else [slice(0, CB)]
-            for span in spans:
-                nc.vector.tensor_scalar(neg_xd[:, span, :], xd_t[:, span, :], -1.0, None, ALU.mult)
-                if c % GROUP == (GROUP - 1 + 2) % GROUP:
-                    nc.vector.tensor_tensor(xd_sq[:, span, :], xd_t[:, span, :], xd_t[:, span, :], ALU.mult)
-                else:
-                    nc.scalar.activation(xd_sq[:, span, :], xd_t[:, span, :], ACT.Square)
-                for cb in range(span.start, span.stop):
-                    nc.vector.tensor_tensor(
-                        d[:, cb, :], table[cb][:].indirect(picked), neg_xd[:, cb, :], ALU.add)
-                nc.vector.tensor_tensor(xs_bf[:, span, :], d[:, span, :], xd_t[:, span, :], ALU.add)
-                nc.vector.tensor_tensor(xs_sq[:, span, :], xs_bf[:, span, :], xs_bf[:, span, :], ALU.mult)
-                nc.vector.tensor_copy(d_bf[:, span, :], d[:, span, :])
-                for cb in range(span.start, span.stop):
-                    nc.vector.tensor_tensor(
-                        p[:, cb, :], table[cb][:].indirect(picked), xd_t[:, cb, :], ALU.mult)
-                nc.vector.tensor_copy(p_bf[:, span, :], p[:, span, :])
-            operands[c] = {"xs": xs_bf, "d": d_bf, "p": p_bf, "xs_sq": xs_sq, "xd_sq": xd_sq}
+            made = operands[c]
+            nc.vector.tensor_scalar(made["neg_xd"][:, span, :], xd_t[:, span, :], -1.0, None, ALU.mult)
+            xd_sq = made["xd_sq"]
+            nc.scalar.activation(xd_sq[:, span, :], xd_t[:, span, :], ACT.Square)
+            d = picked_tile("d")
+            for cb in range(span.start, span.stop):
+                nc.vector.tensor_tensor(
+                    d[:, cb, :], table[cb][:].indirect(picked), made["neg_xd"][:, cb, :], ALU.add)
+            nc.vector.tensor_tensor(made["xs"][:, span, :], d[:, span, :], xd_t[:, span, :], ALU.add)
+            nc.vector.tensor_tensor(made["xs_sq"][:, span, :], made["xs"][:, span, :], made["xs"][:, span, :], ALU.mult)
+            nc.vector.tensor_copy(made["d"][:, span, :], d[:, span, :])
+
+        def make_product(c, span):
+            picked = offsets[:, c * W // 16:(c + 1) * W // 16]
+            xd_t = xd_tiles[c]
+            p = picked_tile("p")
+            for cb in range(span.start, span.stop):
+                nc.vector.tensor_tensor(
+                    p[:, cb, :], table[cb][:].indirect(picked), xd_t[:, cb, :], ALU.mult)
+            nc.vector.tensor_copy(operands[c]["p"][:, span, :], p[:, span, :])
+
+        def make_operands(c, between=None):
+            operands[c] = {
+                "neg_xd": stream.tile([P, CB, W], F32, name="neg_xd"),
+                "xd_sq": stream.tile([P, CB, W], BF16, name="xd_sq", bufs=GROUP + 3),
+                "xs": stream.tile([P, CB, W], BF16, name="xs_bf"),
+                "xs_sq": stream.tile([P, CB, W], BF16, name="xs_sq", bufs=GROUP + 3),
+                "d": stream.tile([P, CB, W], BF16, name="d_bf"),
+                "p": stream.tile([P, CB, W], BF16, name="p_bf", bufs=GROUP + 3),
+            }
+            for span in spans_of(c):
+                make_difference(c, span)
+                if between is not None:
+                    between()
+                make_product(c, span)
 
         def relu(out_ap, acc, bias_column, by_vector):
             if by_vector:
@@ -172,7 +187,7 @@ def tile_edgeattrs_b_kernel(
             nc.scalar.activation(inv_s[:], sums_s[:], ACT.Abs_reciprocal_sqrt)
             inv_d = cosine.tile([P, W], F32, name="inv_d")
             nc.scalar.activation(inv_d[:], sums_d[:], ACT.Abs_reciprocal_sqrt)
-            inverse = cosine.tile([P, W], F32, name="inverse")
+            inverse = stream.tile([P, W], F32, name="inverse", tag="picked", bufs=2)
             nc.vector.tensor_tensor(inverse[:], inv_s[:], inv_d[:], ALU.mult)
             inverses[g] = inverse
 
@@ -221,11 +236,12 @@ def tile_edgeattrs_b_kernel(
         for step in range(CHUNKS - 1):
             if step + 3 < CHUNKS:
                 fetch_xd(step + 3)
-            if step + 2 < CHUNKS:
-                make_operands(step + 2)
-            if step % GROUP == GROUP - 1:
+            def cosines_now():
                 group_norms(step // GROUP)
                 group_cosines(step // GROUP, vector_is_free=False)
+
+            if step + 2 < CHUNKS:
+                make_operands(step + 2, between=cosines_now if step % GROUP == GROUP - 1 else None)
             if step - 2 >= CHUNKS - GROUP:
                 open_final(step - 2)
             first_layer(step, branches[0])

@@ -116,7 +116,10 @@ def tile_edgeattrs_b_kernel(
             picked = offsets[:, c * W // 16:(c + 1) * W // 16]
             xd_t = xd_tiles[c]
             made = operands[c]
-            nc.vector.tensor_scalar(made["neg_xd"][:, span, :], xd_t[:, span, :], -1.0, None, ALU.mult)
+            if c % GROUP == 0:
+                nc.scalar.activation(made["neg_xd"][:, span, :], xd_t[:, span, :], ACT.Copy, scale=-1.0)
+            else:
+                nc.vector.tensor_scalar(made["neg_xd"][:, span, :], xd_t[:, span, :], -1.0, None, ALU.mult)
             xd_sq = made["xd_sq"]
             nc.scalar.activation(xd_sq[:, span, :], xd_t[:, span, :], ACT.Square)
             d = picked_tile("d")
@@ -248,9 +251,11 @@ def tile_edgeattrs_b_kernel(
             first_layer(step, branches[1])
             if step >= 1:
                 second_layer(step - 1, 2)
-            if step >= FINAL_LAG:
-                open_final(step - FINAL_LAG)
-                close_final(step - FINAL_LAG)
+            g, turn = divmod(step - FINAL_LAG, GROUP)
+            if g >= 0 and turn < 2:
+                for c in (g * GROUP + 2 * turn, g * GROUP + 2 * turn + 1):
+                    open_final(c)
+                    close_final(c)
             first_layer(step, branches[2])
             second_layer(step, 0)
             second_layer(step, 1)
@@ -260,13 +265,13 @@ def tile_edgeattrs_b_kernel(
         group_norms(last // GROUP)
         first_layer(last, branches[2], by_vector=True)
         group_cosines(last // GROUP, vector_is_free=True)
+        second_layer(last - 1, 2)
+        open_final(last - 2)
+        close_final(last - 3)
+        close_final(last - 2)
         for b in range(len(branches)):
             second_layer(last, b, by_vector=True)
-        second_layer(last - 1, 2)
-        for c in range(last - FINAL_LAG, CHUNKS - GROUP):
-            open_final(c)
-            close_final(c)
-        for c in range(last - 2, CHUNKS):
-            open_final(c)
-        for c in range(CHUNKS - GROUP, CHUNKS):
-            close_final(c)
+        open_final(last - 1)
+        close_final(last - 1)
+        open_final(last)
+        close_final(last)

@@ -116,7 +116,7 @@ def tile_edgeattrs_b_kernel(
             picked = offsets[:, c * W // 16:(c + 1) * W // 16]
             xd_t = xd_tiles[c]
             made = operands[c]
-            if c % GROUP == 0:
+            if c < FINAL_LAG:
                 nc.scalar.activation(made["neg_xd"][:, span, :], xd_t[:, span, :], ACT.Copy, scale=-1.0)
             else:
                 nc.vector.tensor_scalar(made["neg_xd"][:, span, :], xd_t[:, span, :], -1.0, None, ALU.mult)

@@ -232,6 +232,12 @@ def tile_edgeattrs_b_kernel(
             nc.scalar.activation(out_t[:], acc[:], ACT.Tanh, bias=bfin_t[:, 0:1])
             nc.sync.dma_start(out[:, c * W:(c + 1) * W], out_t[:])
 
+        def final_pair(step):
+            g, turn = divmod(step - FINAL_LAG, GROUP)
+            if g < 0 or turn >= 2:
+                return ()
+            return (g * GROUP + 2 * turn, g * GROUP + 2 * turn + 1)
+
         make_operands(0)
         fetch_xd(2)
         make_operands(1)
@@ -251,27 +257,26 @@ def tile_edgeattrs_b_kernel(
             first_layer(step, branches[1])
             if step >= 1:
                 second_layer(step - 1, 2)
-            g, turn = divmod(step - FINAL_LAG, GROUP)
-            if g >= 0 and turn < 2:
-                for c in (g * GROUP + 2 * turn, g * GROUP + 2 * turn + 1):
-                    open_final(c)
-                    close_final(c)
+            for c in final_pair(step):
+                close_final(c)
+            for c in final_pair(step + 1):
+                open_final(c)
             first_layer(step, branches[2])
             second_layer(step, 0)
             second_layer(step, 1)
         last = CHUNKS - 1
-        first_layer(last, branches[0], by_vector=True)
-        first_layer(last, branches[1], by_vector=True)
+        open_final(last - 2)
+        first_layer(last, branches[0])
+        first_layer(last, branches[1])
+        second_layer(last - 1, 2)
         group_norms(last // GROUP)
+        second_layer(last, 0)
         first_layer(last, branches[2], by_vector=True)
         group_cosines(last // GROUP, vector_is_free=True)
-        second_layer(last - 1, 2)
-        open_final(last - 2)
-        close_final(last - 3)
-        close_final(last - 2)
-        for b in range(len(branches)):
-            second_layer(last, b, by_vector=True)
+        second_layer(last, 1)
         open_final(last - 1)
-        close_final(last - 1)
+        second_layer(last, 2, by_vector=True)
+        for c in range(last - 3, last):
+            close_final(c)
         open_final(last)
         close_final(last)

@@ -116,7 +116,7 @@ def tile_edgeattrs_b_kernel(
             picked = offsets[:, c * W // 16:(c + 1) * W // 16]
             xd_t = xd_tiles[c]
             made = operands[c]
-            if c < FINAL_LAG:
+            if c < FINAL_LAG or c % GROUP == 0:
                 nc.scalar.activation(made["neg_xd"][:, span, :], xd_t[:, span, :], ACT.Copy, scale=-1.0)
             else:
                 nc.vector.tensor_scalar(made["neg_xd"][:, span, :], xd_t[:, span, :], -1.0, None, ALU.mult)

@@ -116,7 +116,7 @@ def tile_edgeattrs_b_kernel(
             picked = offsets[:, c * W // 16:(c + 1) * W // 16]
             xd_t = xd_tiles[c]
             made = operands[c]
-            if c < FINAL_LAG or c % GROUP == 0:
+            if c <= FINAL_LAG or c % GROUP == 0:
                 nc.scalar.activation(made["neg_xd"][:, span, :], xd_t[:, span, :], ACT.Copy, scale=-1.0)
             else:
                 nc.vector.tensor_scalar(made["neg_xd"][:, span, :], xd_t[:, span, :], -1.0, None, ALU.mult)

@@ -270,10 +270,10 @@ def tile_edgeattrs_b_kernel(
         first_layer(last, branches[1])
         second_layer(last - 1, 2)
         group_norms(last // GROUP)
-        second_layer(last, 0)
+        second_layer(last, 0, by_vector=True)
         first_layer(last, branches[2], by_vector=True)
         group_cosines(last // GROUP, vector_is_free=True)
-        second_layer(last, 1)
+        second_layer(last, 1, by_vector=True)
         open_final(last - 1)
         second_layer(last, 2, by_vector=True)
         for c in range(last - 3, last):

@@ -18,6 +18,7 @@ GROUP = 4
 QUAD = P // GROUP
 TABLE_PIECES = 4
 FINAL_LAG = GROUP + 1
+TURN_TILES = 12
 
 FLOPS = 2 * N * (3 * C * F + 3 * F * O + Z * O)
 
@@ -109,35 +110,37 @@ def tile_edgeattrs_b_kernel(
         def spans_of(c):
             return [slice(cb, cb + 1) for cb in range(CB)] if c == 0 else [slice(0, CB)]
 
-        def picked_tile(name):
-            return stream.tile([P, CB, W], F32, name=name, tag="picked", bufs=2)
+        def turn_tile(shape, dtype, name):
+            return stream.tile(shape, dtype, name=name, tag="turn", bufs=TURN_TILES)
 
         def make_difference(c, span):
             picked = offsets[:, c * W // 16:(c + 1) * W // 16]
             xd_t = xd_tiles[c]
             made = operands[c]
-            if c <= FINAL_LAG or c % GROUP == 0:
+            if c < 2:
                 nc.scalar.activation(made["neg_xd"][:, span, :], xd_t[:, span, :], ACT.Copy, scale=-1.0)
             else:
                 nc.vector.tensor_scalar(made["neg_xd"][:, span, :], xd_t[:, span, :], -1.0, None, ALU.mult)
             xd_sq = made["xd_sq"]
             nc.scalar.activation(xd_sq[:, span, :], xd_t[:, span, :], ACT.Square)
-            d = picked_tile("d")
+            if "d" not in made:
+                made["d"] = turn_tile([P, CB, W], F32, "d")
+            d = made["d"]
             for cb in range(span.start, span.stop):
                 nc.vector.tensor_tensor(
                     d[:, cb, :], table[cb][:].indirect(picked), made["neg_xd"][:, cb, :], ALU.add)
             nc.vector.tensor_tensor(made["xs"][:, span, :], d[:, span, :], xd_t[:, span, :], ALU.add)
             nc.vector.tensor_tensor(made["xs_sq"][:, span, :], made["xs"][:, span, :], made["xs"][:, span, :], ALU.mult)
-            nc.vector.tensor_copy(made["d"][:, span, :], d[:, span, :])
 
         def make_product(c, span):
             picked = offsets[:, c * W // 16:(c + 1) * W // 16]
             xd_t = xd_tiles[c]
-            p = picked_tile("p")
+            if "p" not in operands[c]:
+                operands[c]["p"] = turn_tile([P, CB, W], F32, "p")
+            p = operands[c]["p"]
             for cb in range(span.start, span.stop):
                 nc.vector.tensor_tensor(
                     p[:, cb, :], table[cb][:].indirect(picked), xd_t[:, cb, :], ALU.mult)
-            nc.vector.tensor_copy(operands[c]["p"][:, span, :], p[:, span, :])
 
         def make_operands(c, between=None):
             operands[c] = {
@@ -145,14 +148,18 @@ def tile_edgeattrs_b_kernel(
                 "xd_sq": stream.tile([P, CB, W], BF16, name="xd_sq", bufs=GROUP + 3),
                 "xs": stream.tile([P, CB, W], BF16, name="xs_bf"),
                 "xs_sq": stream.tile([P, CB, W], BF16, name="xs_sq", bufs=GROUP + 3),
-                "d": stream.tile([P, CB, W], BF16, name="d_bf"),
-                "p": stream.tile([P, CB, W], BF16, name="p_bf", bufs=GROUP + 3),
             }
             for span in spans_of(c):
                 make_difference(c, span)
                 if between is not None:
                     between()
                 make_product(c, span)
+
+        def as_bf16(tile, cb):
+            block = tile[:, cb, :]
+            if tile.dtype == F32:
+                block = block.bitcast(BF16)[:, 1::2]
+            return block
 
         def relu(out_ap, acc, bias_column, by_vector):
             if by_vector:
@@ -168,7 +175,7 @@ def tile_edgeattrs_b_kernel(
                 acc = banks.tile([P, W], F32, name="acc")
                 for cb in range(CB):
                     nc.tensor.matmul(
-                        acc[:], wa_t[:, cb, fb * P:(fb + 1) * P], h[:, cb, :],
+                        acc[:], wa_t[:, cb, fb * P:(fb + 1) * P], as_bf16(h, cb),
                         start=cb == 0, stop=cb == CB - 1)
                 relu(u[:, fb, :], acc, ba_t[:, fb:fb + 1], by_vector)
             operands[c]["u_" + name] = u
@@ -179,7 +186,7 @@ def tile_edgeattrs_b_kernel(
                 for cb in range(CB):
                     nc.tensor.matmul(
                         sums[q * QUAD:(q + 1) * QUAD, :], ones[:],
-                        operands[g * GROUP + q][name][:, cb, :],
+                        as_bf16(operands[g * GROUP + q][name], cb),
                         start=cb == 0, stop=cb == CB - 1)
             return sums
 
@@ -190,7 +197,7 @@ def tile_edgeattrs_b_kernel(
             nc.scalar.activation(inv_s[:], sums_s[:], ACT.Abs_reciprocal_sqrt)
             inv_d = cosine.tile([P, W], F32, name="inv_d")
             nc.scalar.activation(inv_d[:], sums_d[:], ACT.Abs_reciprocal_sqrt)
-            inverse = stream.tile([P, W], F32, name="inverse", tag="picked", bufs=2)
+            inverse = turn_tile([P, W], F32, "inverse")
             nc.vector.tensor_tensor(inverse[:], inv_s[:], inv_d[:], ALU.mult)
             inverses[g] = inverse
 
@@ -200,7 +207,7 @@ def tile_edgeattrs_b_kernel(
                 dot_copy = cosine.tile([P, W], F32, name="dot_copy")
                 nc.scalar.copy(dot_copy[:], dot[:])
                 dot = dot_copy
-            cs_bf = cosine.tile([P, W], BF16, name="cs_bf")
+            cs_bf = turn_tile([P, W], BF16, "cs_bf")
             nc.vector.tensor_tensor(cs_bf[:], dot[:], inverses[g][:], ALU.mult)
             cosines[g] = cs_bf
 

@@ -58,7 +58,8 @@ def tile_edgeattrs_b_kernel(
             for k in range(TABLE_PIECES):
                 columns = slice(k * S // TABLE_PIECES, (k + 1) * S // TABLE_PIECES)
                 nc.sync.dma_start(table[cb][:, columns], x[cb * P:(cb + 1) * P, columns])
-        fetch_xd(1)
+            if cb == 0:
+                fetch_xd(1)
 
         def first_weight(w, name):
             return load(nc.sync, [P, CB, F], BF16, w.rearrange("(cb p) f -> p cb f", p=P), name)
@@ -107,9 +108,6 @@ def tile_edgeattrs_b_kernel(
         cosines = {}
         open_banks = {}
 
-        def spans_of(c):
-            return [slice(cb, cb + 1) for cb in range(CB)] if c == 0 else [slice(0, CB)]
-
         def turn_tile(shape, dtype, name):
             return stream.tile(shape, dtype, name=name, tag="turn", bufs=TURN_TILES)
 
@@ -122,7 +120,10 @@ def tile_edgeattrs_b_kernel(
             else:
                 nc.vector.tensor_scalar(made["neg_xd"][:, span, :], xd_t[:, span, :], -1.0, None, ALU.mult)
             xd_sq = made["xd_sq"]
-            nc.scalar.activation(xd_sq[:, span, :], xd_t[:, span, :], ACT.Square)
+            if c >= GROUP and c % GROUP == 1:
+                nc.vector.tensor_tensor(xd_sq[:, span, :], xd_t[:, span, :], xd_t[:, span, :], ALU.mult)
+            else:
+                nc.scalar.activation(xd_sq[:, span, :], xd_t[:, span, :], ACT.Square)
             if "d" not in made:
                 made["d"] = turn_tile([P, CB, W], F32, "d")
             d = made["d"]
@@ -142,18 +143,20 @@ def tile_edgeattrs_b_kernel(
                 nc.vector.tensor_tensor(
                     p[:, cb, :], table[cb][:].indirect(picked), xd_t[:, cb, :], ALU.mult)
 
-        def make_operands(c, between=None):
+        def new_operands(c):
             operands[c] = {
                 "neg_xd": stream.tile([P, CB, W], F32, name="neg_xd"),
                 "xd_sq": stream.tile([P, CB, W], BF16, name="xd_sq", bufs=GROUP + 3),
                 "xs": stream.tile([P, CB, W], BF16, name="xs_bf"),
                 "xs_sq": stream.tile([P, CB, W], BF16, name="xs_sq", bufs=GROUP + 3),
             }
-            for span in spans_of(c):
-                make_difference(c, span)
-                if between is not None:
-                    between()
-                make_product(c, span)
+
+        def make_operands(c, between=None):
+            new_operands(c)
+            make_difference(c, slice(0, CB))
+            if between is not None:
+                between()
+            make_product(c, slice(0, CB))
 
         def as_bf16(tile, cb):
             block = tile[:, cb, :]
@@ -245,9 +248,13 @@ def tile_edgeattrs_b_kernel(
                 return ()
             return (g * GROUP + 2 * turn, g * GROUP + 2 * turn + 1)
 
-        make_operands(0)
         fetch_xd(2)
-        make_operands(1)
+        for c in (0, 1):
+            new_operands(c)
+        for cb in range(CB):
+            for c in (0, 1):
+                make_difference(c, slice(cb, cb + 1))
+                make_product(c, slice(cb, cb + 1))
         edge_t = load(nc.sync, [P, N], BF16, edge_attr, "edge_t")
         for step in range(CHUNKS - 1):
             if step + 3 < CHUNKS:

@@ -44,6 +44,27 @@ def tile_edgeattrs_b_kernel(
 
         offsets = held.tile([P, N // 16], U16, name="offsets")
         nc.sync.dma_start(offsets[:], offs)
+        ones = held.tile([P, QUAD], BF16, name="ones")
+        nc.vector.memset(ones[:], 1.0)
+
+        identity = held.tile([P, P], F32, name="identity")
+        make_identity(nc, identity[:])
+        ws_rows = load(nc.scalar, [P, O], F32,
+                       ws.rearrange("o one -> (o one)").partition_broadcast(P), "ws_rows")
+        ws_high = held.tile([P, O], BF16, name="ws_high")
+        nc.vector.tensor_copy(ws_high[:], ws_rows[:])
+        ws_low = held.tile([P, O], BF16, name="ws_low")
+        nc.vector.tensor_tensor(ws_low[:], ws_rows[:], ws_high[:], ALU.subtract)
+        ws_of_chunk = held.tile([P, GROUP, O], BF16, name="ws_of_chunk")
+        for q in range(GROUP):
+            row = q * QUAD
+            high_row = held.tile([P, O], BF16, name="high_row%d" % q)
+            nc.vector.tensor_scalar(high_row[:], ws_high[:], identity[:, row:row + 1], None, ALU.mult)
+            nc.vector.scalar_tensor_tensor(
+                ws_of_chunk[:, q, :], ws_low[:], identity[:, row + 1:row + 2], high_row[:],
+                ALU.mult, ALU.add,
+            )
+
         xd_blocks = xd.rearrange("(cb p) n -> p cb n", p=P)
         xd_tiles = {}
 
@@ -80,27 +101,6 @@ def tile_edgeattrs_b_kernel(
         )
         wf_t = load(nc.sync, [P, ZB, O], BF16, wf.rearrange("(zb p) o -> p zb o", p=P), "wf_t")
         bfin_t = bias(bfin, 1, "bfin_t")
-
-        ones = held.tile([P, QUAD], BF16, name="ones")
-        nc.vector.memset(ones[:], 1.0)
-
-        identity = held.tile([P, P], F32, name="identity")
-        make_identity(nc, identity[:])
-        ws_rows = load(nc.scalar, [P, O], F32,
-                       ws.rearrange("o one -> (o one)").partition_broadcast(P), "ws_rows")
-        ws_high = held.tile([P, O], BF16, name="ws_high")
-        nc.vector.tensor_copy(ws_high[:], ws_rows[:])
-        ws_low = held.tile([P, O], BF16, name="ws_low")
-        nc.vector.tensor_tensor(ws_low[:], ws_rows[:], ws_high[:], ALU.subtract)
-        ws_of_chunk = held.tile([P, GROUP, O], BF16, name="ws_of_chunk")
-        for q in range(GROUP):
-            row = q * QUAD
-            high_row = held.tile([P, O], BF16, name="high_row%d" % q)
-            nc.vector.tensor_scalar(high_row[:], ws_high[:], identity[:, row:row + 1], None, ALU.mult)
-            nc.vector.scalar_tensor_tensor(
-                ws_of_chunk[:, q, :], ws_low[:], identity[:, row + 1:row + 2], high_row[:],
-                ALU.mult, ALU.add,
-            )
 
         operands = {}
         outputs = {}

@@ -102,6 +102,10 @@ def tile_edgeattrs_b_kernel(
         wf_t = load(nc.sync, [P, ZB, O], BF16, wf.rearrange("(zb p) o -> p zb o", p=P), "wf_t")
         bfin_t = bias(bfin, 1, "bfin_t")
 
+        first_set = held.tile([P, 1], F32, name="first_set")
+        nc.vector.memset(first_set[:], 1.0)
+        nc.scalar.activation(first_set[:], first_set[:], ACT.Abs_reciprocal_sqrt)
+
         operands = {}
         outputs = {}
         inverses = {}

@@ -68,19 +68,10 @@ def tile_edgeattrs_b_kernel(
         xd_blocks = xd.rearrange("(cb p) n -> p cb n", p=P)
         xd_tiles = {}
 
-        def fetch_xd(c):
-            xd_t = stream.tile([P, CB, W], F32, name="xd_t", bufs=4)
-            nc.sync.dma_start(xd_t[:], xd_blocks[:, :, c * W:(c + 1) * W])
-            xd_tiles[c] = xd_t
-
-        fetch_xd(0)
-        table = [held.tile([P, S], F32, name="table%d" % cb) for cb in range(CB)]
-        for cb in range(CB):
-            for k in range(TABLE_PIECES):
-                columns = slice(k * S // TABLE_PIECES, (k + 1) * S // TABLE_PIECES)
-                nc.sync.dma_start(table[cb][:, columns], x[cb * P:(cb + 1) * P, columns])
-            if cb == 0:
-                fetch_xd(1)
+        def fetch_xd(c, span=slice(0, CB)):
+            if c not in xd_tiles:
+                xd_tiles[c] = stream.tile([P, CB, W], F32, name="xd_t", bufs=4)
+            nc.sync.dma_start(xd_tiles[c][:, span, :], xd_blocks[:, span, c * W:(c + 1) * W])
 
         def first_weight(w, name):
             return load(nc.sync, [P, CB, F], BF16, w.rearrange("(cb p) f -> p cb f", p=P), name)
@@ -91,12 +82,24 @@ def tile_edgeattrs_b_kernel(
         def bias(b, blocks, name):
             return load(nc.scalar, [P, blocks], F32, b.rearrange("(a p) o -> p (a o)", p=P), name)
 
+        table = [held.tile([P, S], F32, name="table%d" % cb) for cb in range(CB)]
+        first_weights = []
+        for cb in range(CB):
+            fetch_xd(0, slice(cb, cb + 1))
+            for k in range(TABLE_PIECES):
+                columns = slice(k * S // TABLE_PIECES, (k + 1) * S // TABLE_PIECES)
+                nc.sync.dma_start(table[cb][:, columns], x[cb * P:(cb + 1) * P, columns])
+            fetch_xd(1, slice(cb, cb + 1))
+            if cb == 0:
+                first_weights.extend((first_weight(w1a, "w1a_t"), first_weight(w3a, "w3a_t"),
+                                      first_weight(w4a, "w4a_t")))
+
         branches = (
-            ("xs", first_weight(w1a, "w1a_t"), bias(b1a, FB, "b1a_t"),
+            ("xs", first_weights[0], bias(b1a, FB, "b1a_t"),
              second_weight(w1b, "w1b_t"), bias(b1b, 1, "b1b_t")),
-            ("d", first_weight(w3a, "w3a_t"), bias(b3a, FB, "b3a_t"),
+            ("d", first_weights[1], bias(b3a, FB, "b3a_t"),
              second_weight(w3b, "w3b_t"), bias(b3b, 1, "b3b_t")),
-            ("p", first_weight(w4a, "w4a_t"), bias(b4a, FB, "b4a_t"),
+            ("p", first_weights[2], bias(b4a, FB, "b4a_t"),
              second_weight(w4b, "w4b_t"), bias(b4b, 1, "b4b_t")),
         )
         wf_t = load(nc.sync, [P, ZB, O], BF16, wf.rearrange("(zb p) o -> p zb o", p=P), "wf_t")
@@ -174,17 +177,26 @@ def tile_edgeattrs_b_kernel(
             else:
                 nc.scalar.activation(out_ap, acc[:], ACT.Relu, bias=bias_column)
 
-        def first_layer(c, branch, by_vector=False):
+        half_sums = {}
+
+        def first_layer_block(c, branch, cb):
             name, wa_t, ba_t, wb_t, bb_t = branch
             h = operands[c][name]
+            if cb == 0:
+                half_sums[c, name] = [banks.tile([P, W], F32, name="acc") for fb in range(FB)]
+            for fb in range(FB):
+                nc.tensor.matmul(
+                    half_sums[c, name][fb][:], wa_t[:, cb, fb * P:(fb + 1) * P], as_bf16(h, cb),
+                    start=cb == 0, stop=cb == CB - 1)
+
+        def first_layer(c, branch, by_vector=False):
+            name, wa_t, ba_t, wb_t, bb_t = branch
+            for cb in range(CB):
+                if cb > 0 or (c, name) not in half_sums:
+                    first_layer_block(c, branch, cb)
             u = hidden.tile([P, FB, W], BF16, name="u")
             for fb in range(FB):
-                acc = banks.tile([P, W], F32, name="acc")
-                for cb in range(CB):
-                    nc.tensor.matmul(
-                        acc[:], wa_t[:, cb, fb * P:(fb + 1) * P], as_bf16(h, cb),
-                        start=cb == 0, stop=cb == CB - 1)
-                relu(u[:, fb, :], acc, ba_t[:, fb:fb + 1], by_vector)
+                relu(u[:, fb, :], half_sums[c, name][fb], ba_t[:, fb:fb + 1], by_vector)
             operands[c]["u_" + name] = u
 
         def group_sums(g, name):
@@ -259,6 +271,9 @@ def tile_edgeattrs_b_kernel(
             for c in (0, 1):
                 make_difference(c, slice(cb, cb + 1))
                 make_product(c, slice(cb, cb + 1))
+            if cb == 0:
+                for branch in branches:
+                    first_layer_block(0, branch, 0)
         edge_t = load(nc.sync, [P, N], BF16, edge_attr, "edge_t")
         for step in range(CHUNKS - 1):
             if step + 3 < CHUNKS:

@@ -127,7 +127,7 @@ def tile_edgeattrs_b_kernel(
             else:
                 nc.vector.tensor_scalar(made["neg_xd"][:, span, :], xd_t[:, span, :], -1.0, None, ALU.mult)
             xd_sq = made["xd_sq"]
-            if c >= GROUP and c % GROUP == 1:
+            if c >= 2 * GROUP and c % GROUP == 1:
                 nc.vector.tensor_tensor(xd_sq[:, span, :], xd_t[:, span, :], xd_t[:, span, :], ALU.mult)
             else:
                 nc.scalar.activation(xd_sq[:, span, :], xd_t[:, span, :], ACT.Square)

@@ -93,6 +93,7 @@ def tile_edgeattrs_b_kernel(
             if cb == 0:
                 first_weights.extend((first_weight(w1a, "w1a_t"), first_weight(w3a, "w3a_t"),
                                       first_weight(w4a, "w4a_t")))
+        fetch_xd(2)
 
         branches = (
             ("xs", first_weights[0], bias(b1a, FB, "b1a_t"),
@@ -122,7 +123,7 @@ def tile_edgeattrs_b_kernel(
             picked = offsets[:, c * W // 16:(c + 1) * W // 16]
             xd_t = xd_tiles[c]
             made = operands[c]
-            if c < 2:
+            if c < 3:
                 nc.scalar.activation(made["neg_xd"][:, span, :], xd_t[:, span, :], ACT.Copy, scale=-1.0)
             else:
                 nc.vector.tensor_scalar(made["neg_xd"][:, span, :], xd_t[:, span, :], -1.0, None, ALU.mult)
@@ -138,7 +139,8 @@ def tile_edgeattrs_b_kernel(
                 nc.vector.tensor_tensor(
                     d[:, cb, :], table[cb][:].indirect(picked), made["neg_xd"][:, cb, :], ALU.add)
             nc.vector.tensor_tensor(made["xs"][:, span, :], d[:, span, :], xd_t[:, span, :], ALU.add)
-            nc.vector.tensor_tensor(made["xs_sq"][:, span, :], made["xs"][:, span, :], made["xs"][:, span, :], ALU.mult)
+            if not (c < 2 and span.stop == 1):
+                nc.vector.tensor_tensor(made["xs_sq"][:, span, :], made["xs"][:, span, :], made["xs"][:, span, :], ALU.mult)
 
         def make_product(c, span):
             picked = offsets[:, c * W // 16:(c + 1) * W // 16]
@@ -264,7 +266,6 @@ def tile_edgeattrs_b_kernel(
                 return ()
             return (g * GROUP + 2 * turn, g * GROUP + 2 * turn + 1)
 
-        fetch_xd(2)
         for c in (0, 1):
             new_operands(c)
         for cb in range(CB):
@@ -272,6 +273,8 @@ def tile_edgeattrs_b_kernel(
                 make_difference(c, slice(cb, cb + 1))
                 make_product(c, slice(cb, cb + 1))
             if cb == 0:
+                for c in (0, 1):
+                    nc.scalar.activation(operands[c]["xs_sq"][:, cb, :], operands[c]["xs"][:, cb, :], ACT.Square)
                 for branch in branches:
                     first_layer_block(0, branch, 0)
         edge_t = load(nc.sync, [P, N], BF16, edge_attr, "edge_t")

@@ -222,12 +222,15 @@ def tile_edgeattrs_b_kernel(
             nc.vector.tensor_tensor(inverse[:], inv_s[:], inv_d[:], ALU.mult)
             inverses[g] = inverse
 
-        def group_cosines(g, vector_is_free):
+        def group_products(g, vector_is_free):
             dot = group_sums(g, "p")
             if not vector_is_free:
                 dot_copy = cosine.tile([P, W], F32, name="dot_copy")
                 nc.scalar.copy(dot_copy[:], dot[:])
                 dot = dot_copy
+            return dot
+
+        def group_cosines(g, dot):
             cs_bf = turn_tile([P, W], BF16, "cs_bf")
             nc.vector.tensor_tensor(cs_bf[:], dot[:], inverses[g][:], ALU.mult)
             cosines[g] = cs_bf
@@ -282,8 +285,9 @@ def tile_edgeattrs_b_kernel(
             if step + 3 < CHUNKS:
                 fetch_xd(step + 3)
             def cosines_now():
+                dot = group_products(step // GROUP, vector_is_free=False)
                 group_norms(step // GROUP)
-                group_cosines(step // GROUP, vector_is_free=False)
+                group_cosines(step // GROUP, dot)
 
             if step + 2 < CHUNKS:
                 make_operands(step + 2, between=cosines_now if step % GROUP == GROUP - 1 else None)
@@ -308,7 +312,7 @@ def tile_edgeattrs_b_kernel(
         group_norms(last // GROUP)
         second_layer(last, 0, by_vector=True)
         first_layer(last, branches[2], by_vector=True)
-        group_cosines(last // GROUP, vector_is_free=True)
+        group_cosines(last // GROUP, group_products(last // GROUP, vector_is_free=True))
         second_layer(last, 1, by_vector=True)
         open_final(last - 1)
         second_layer(last, 2, by_vector=True)

@@ -80,7 +80,7 @@ def tile_edgeattrs_b_kernel(
             return load(nc.sync, [P, FB, O], BF16, w.rearrange("(fb p) o -> p fb o", p=P), name)
 
         def bias(b, blocks, name):
-            return load(nc.scalar, [P, blocks], F32, b.rearrange("(a p) o -> p (a o)", p=P), name)
+            return load(nc.sync, [P, blocks], F32, b.rearrange("(a p) o -> p (a o)", p=P), name)
 
         table = [held.tile([P, S], F32, name="table%d" % cb) for cb in range(CB)]
         first_weights = []

@@ -18,7 +18,7 @@ GROUP = 4
 QUAD = P // GROUP
 TABLE_PIECES = 4
 FINAL_LAG = GROUP + 1
-TURN_TILES = 12
+TURN_TILES = 14
 
 FLOPS = 2 * N * (3 * C * F + 3 * F * O + Z * O)
 
@@ -32,7 +32,7 @@ def tile_edgeattrs_b_kernel(
     with (
         tc.tile_pool(name="held", bufs=1) as held,
         tc.tile_pool(name="stream", bufs=3) as stream,
-        tc.tile_pool(name="hidden", bufs=6) as hidden,
+        tc.tile_pool(name="hidden", bufs=8) as hidden,
         tc.tile_pool(name="late", bufs=FINAL_LAG + 2) as late,
         tc.tile_pool(name="cosine", bufs=2) as cosine,
         tc.psum_pool(name="banks", bufs=8) as banks,

import concourse.mybir as mybir
from concourse.masks import make_identity

F32 = mybir.dt.float32
BF16 = mybir.dt.bfloat16
U16 = mybir.dt.uint16
ALU = mybir.AluOpType
ACT = mybir.ActivationFunctionType

P = 128
C, F, O, Z, S, N = 256, 256, 128, 512, 4096, 8192
CB = C // P
FB = F // P
ZB = Z // P
W = 512
CHUNKS = N // W
GROUP = 4
QUAD = P // GROUP
TABLE_PIECES = 4
FINAL_LAG = GROUP + 1
TURN_TILES = 14

FLOPS = 2 * N * (3 * C * F + 3 * F * O + Z * O)


def tile_edgeattrs_b_kernel(
    tc, x, xd, edge_attr,
    w1a, b1a, w1b, b1b, w3a, b3a, w3b, b3b, w4a, b4a, w4b, b4b,
    wf, ws, bfin, offs, out,
):
    nc = tc.nc
    with (
        tc.tile_pool(name="held", bufs=1) as held,
        tc.tile_pool(name="stream", bufs=3) as stream,
        tc.tile_pool(name="hidden", bufs=8) as hidden,
        tc.tile_pool(name="late", bufs=FINAL_LAG + 2) as late,
        tc.tile_pool(name="cosine", bufs=2) as cosine,
        tc.psum_pool(name="banks", bufs=8) as banks,
    ):
        def load(queue, shape, dtype, source, name):
            tile = held.tile(shape, dtype, name=name)
            queue.dma_start(tile[:], source)
            return tile

        offsets = held.tile([P, N // 16], U16, name="offsets")
        nc.sync.dma_start(offsets[:], offs)
        ones = held.tile([P, QUAD], BF16, name="ones")
        nc.vector.memset(ones[:], 1.0)

        identity = held.tile([P, P], F32, name="identity")
        make_identity(nc, identity[:])
        ws_rows = load(nc.scalar, [P, O], F32,
                       ws.rearrange("o one -> (o one)").partition_broadcast(P), "ws_rows")
        ws_high = held.tile([P, O], BF16, name="ws_high")
        nc.vector.tensor_copy(ws_high[:], ws_rows[:])
        ws_low = held.tile([P, O], BF16, name="ws_low")
        nc.vector.tensor_tensor(ws_low[:], ws_rows[:], ws_high[:], ALU.subtract)
        ws_of_chunk = held.tile([P, GROUP, O], BF16, name="ws_of_chunk")
        for q in range(GROUP):
            row = q * QUAD
            high_row = held.tile([P, O], BF16, name="high_row%d" % q)
            nc.vector.tensor_scalar(high_row[:], ws_high[:], identity[:, row:row + 1], None, ALU.mult)
            nc.vector.scalar_tensor_tensor(
                ws_of_chunk[:, q, :], ws_low[:], identity[:, row + 1:row + 2], high_row[:],
                ALU.mult, ALU.add,
            )

        xd_blocks = xd.rearrange("(cb p) n -> p cb n", p=P)
        xd_tiles = {}

        def fetch_xd(c, span=slice(0, CB)):
            if c not in xd_tiles:
                xd_tiles[c] = stream.tile([P, CB, W], F32, name="xd_t", bufs=4)
            nc.sync.dma_start(xd_tiles[c][:, span, :], xd_blocks[:, span, c * W:(c + 1) * W])

        def first_weight(w, name):
            return load(nc.sync, [P, CB, F], BF16, w.rearrange("(cb p) f -> p cb f", p=P), name)

        def second_weight(w, name):
            return load(nc.sync, [P, FB, O], BF16, w.rearrange("(fb p) o -> p fb o", p=P), name)

        def bias(b, blocks, name):
            return load(nc.sync, [P, blocks], F32, b.rearrange("(a p) o -> p (a o)", p=P), name)

        table = [held.tile([P, S], F32, name="table%d" % cb) for cb in range(CB)]
        first_weights = []
        for cb in range(CB):
            fetch_xd(0, slice(cb, cb + 1))
            for k in range(TABLE_PIECES):
                columns = slice(k * S // TABLE_PIECES, (k + 1) * S // TABLE_PIECES)
                nc.sync.dma_start(table[cb][:, columns], x[cb * P:(cb + 1) * P, columns])
            fetch_xd(1, slice(cb, cb + 1))
            if cb == 0:
                first_weights.extend((first_weight(w1a, "w1a_t"), first_weight(w3a, "w3a_t"),
                                      first_weight(w4a, "w4a_t")))
        fetch_xd(2)

        branches = (
            ("xs", first_weights[0], bias(b1a, FB, "b1a_t"),
             second_weight(w1b, "w1b_t"), bias(b1b, 1, "b1b_t")),
            ("d", first_weights[1], bias(b3a, FB, "b3a_t"),
             second_weight(w3b, "w3b_t"), bias(b3b, 1, "b3b_t")),
            ("p", first_weights[2], bias(b4a, FB, "b4a_t"),
             second_weight(w4b, "w4b_t"), bias(b4b, 1, "b4b_t")),
        )
        wf_t = load(nc.sync, [P, ZB, O], BF16, wf.rearrange("(zb p) o -> p zb o", p=P), "wf_t")
        bfin_t = bias(bfin, 1, "bfin_t")

        first_set = held.tile([P, 1], F32, name="first_set")
        nc.vector.memset(first_set[:], 1.0)
        nc.scalar.activation(first_set[:], first_set[:], ACT.Abs_reciprocal_sqrt)

        operands = {}
        outputs = {}
        inverses = {}
        cosines = {}
        open_banks = {}

        def turn_tile(shape, dtype, name):
            return stream.tile(shape, dtype, name=name, tag="turn", bufs=TURN_TILES)

        def make_difference(c, span):
            picked = offsets[:, c * W // 16:(c + 1) * W // 16]
            xd_t = xd_tiles[c]
            made = operands[c]
            if c < 3:
                nc.scalar.activation(made["neg_xd"][:, span, :], xd_t[:, span, :], ACT.Copy, scale=-1.0)
            else:
                nc.vector.tensor_scalar(made["neg_xd"][:, span, :], xd_t[:, span, :], -1.0, None, ALU.mult)
            xd_sq = made["xd_sq"]
            if c >= 2 * GROUP and c % GROUP == 1:
                nc.vector.tensor_tensor(xd_sq[:, span, :], xd_t[:, span, :], xd_t[:, span, :], ALU.mult)
            else:
                nc.scalar.activation(xd_sq[:, span, :], xd_t[:, span, :], ACT.Square)
            if "d" not in made:
                made["d"] = turn_tile([P, CB, W], F32, "d")
            d = made["d"]
            for cb in range(span.start, span.stop):
                nc.vector.tensor_tensor(
                    d[:, cb, :], table[cb][:].indirect(picked), made["neg_xd"][:, cb, :], ALU.add)
            nc.vector.tensor_tensor(made["xs"][:, span, :], d[:, span, :], xd_t[:, span, :], ALU.add)
            if not (c < 2 and span.stop == 1):
                nc.vector.tensor_tensor(made["xs_sq"][:, span, :], made["xs"][:, span, :], made["xs"][:, span, :], ALU.mult)

        def make_product(c, span):
            picked = offsets[:, c * W // 16:(c + 1) * W // 16]
            xd_t = xd_tiles[c]
            if "p" not in operands[c]:
                operands[c]["p"] = turn_tile([P, CB, W], F32, "p")
            p = operands[c]["p"]
            for cb in range(span.start, span.stop):
                nc.vector.tensor_tensor(
                    p[:, cb, :], table[cb][:].indirect(picked), xd_t[:, cb, :], ALU.mult)

        def new_operands(c):
            operands[c] = {
                "neg_xd": stream.tile([P, CB, W], F32, name="neg_xd"),
                "xd_sq": stream.tile([P, CB, W], BF16, name="xd_sq", bufs=GROUP + 3),
                "xs": stream.tile([P, CB, W], BF16, name="xs_bf"),
                "xs_sq": stream.tile([P, CB, W], BF16, name="xs_sq", bufs=GROUP + 3),
            }

        def make_operands(c, between=None):
            new_operands(c)
            make_difference(c, slice(0, CB))
            if between is not None:
                between()
            make_product(c, slice(0, CB))

        def as_bf16(tile, cb):
            block = tile[:, cb, :]
            if tile.dtype == F32:
                block = block.bitcast(BF16)[:, 1::2]
            return block

        def relu(out_ap, acc, bias_column, by_vector):
            if by_vector:
                nc.vector.tensor_scalar(out_ap, acc[:], bias_column, 0.0, ALU.add, ALU.max)
            else:
                nc.scalar.activation(out_ap, acc[:], ACT.Relu, bias=bias_column)

        half_sums = {}

        def first_layer_block(c, branch, cb):
            name, wa_t, ba_t, wb_t, bb_t = branch
            h = operands[c][name]
            if cb == 0:
                half_sums[c, name] = [banks.tile([P, W], F32, name="acc") for fb in range(FB)]
            for fb in range(FB):
                nc.tensor.matmul(
                    half_sums[c, name][fb][:], wa_t[:, cb, fb * P:(fb + 1) * P], as_bf16(h, cb),
                    start=cb == 0, stop=cb == CB - 1)

        def first_layer(c, branch, by_vector=False):
            name, wa_t, ba_t, wb_t, bb_t = branch
            for cb in range(CB):
                if cb > 0 or (c, name) not in half_sums:
                    first_layer_block(c, branch, cb)
            u = hidden.tile([P, FB, W], BF16, name="u")
            for fb in range(FB):
                relu(u[:, fb, :], half_sums[c, name][fb], ba_t[:, fb:fb + 1], by_vector)
            operands[c]["u_" + name] = u

        def group_sums(g, name):
            sums = banks.tile([P, W], F32, name="acc")
            for q in range(GROUP):
                for cb in range(CB):
                    nc.tensor.matmul(
                        sums[q * QUAD:(q + 1) * QUAD, :], ones[:],
                        as_bf16(operands[g * GROUP + q][name], cb),
                        start=cb == 0, stop=cb == CB - 1)
            return sums

        def group_norms(g):
            sums_s = group_sums(g, "xs_sq")
            sums_d = group_sums(g, "xd_sq")
            inv_s = cosine.tile([P, W], F32, name="inv_s")
            nc.scalar.activation(inv_s[:], sums_s[:], ACT.Abs_reciprocal_sqrt)
            inv_d = cosine.tile([P, W], F32, name="inv_d")
            nc.scalar.activation(inv_d[:], sums_d[:], ACT.Abs_reciprocal_sqrt)
            inverse = turn_tile([P, W], F32, "inverse")
            nc.vector.tensor_tensor(inverse[:], inv_s[:], inv_d[:], ALU.mult)
            inverses[g] = inverse

        def group_products(g, vector_is_free):
            dot = group_sums(g, "p")
            if not vector_is_free:
                dot_copy = cosine.tile([P, W], F32, name="dot_copy")
                nc.scalar.copy(dot_copy[:], dot[:])
                dot = dot_copy
            return dot

        def group_cosines(g, dot):
            cs_bf = turn_tile([P, W], BF16, "cs_bf")
            nc.vector.tensor_tensor(cs_bf[:], dot[:], inverses[g][:], ALU.mult)
            cosines[g] = cs_bf

        def second_layer(c, b, by_vector=False):
            name, wa_t, ba_t, wb_t, bb_t = branches[b]
            if b == 0:
                outputs[c] = late.tile([P, len(branches), W], BF16, name="y")
            u = operands[c]["u_" + name]
            acc = banks.tile([P, W], F32, name="acc")
            for fb in range(FB):
                nc.tensor.matmul(acc[:], wb_t[:, fb, :], u[:, fb, :],
                                 start=fb == 0, stop=fb == FB - 1)
            relu(outputs[c][:, b, :], acc, bb_t[:, 0:1], by_vector)

        def open_final(c):
            y = outputs[c]
            acc = banks.tile([P, W], F32, name="acc")
            nc.tensor.matmul(acc[:], wf_t[:, ZB - 1, :], edge_t[:, c * W:(c + 1) * W],
                             start=True, stop=False)
            for b in range(len(branches)):
                nc.tensor.matmul(acc[:], wf_t[:, b, :], y[:, b, :], start=False, stop=False)
            open_banks[c] = acc

        def close_final(c):
            acc = open_banks[c]
            nc.tensor.matmul(acc[:], ws_of_chunk[:, c % GROUP, :], cosines[c // GROUP][:],
                             start=False, stop=True)
            out_t = stream.tile([P, W], F32, name="out_t", bufs=GROUP + 2)
            nc.scalar.activation(out_t[:], acc[:], ACT.Tanh, bias=bfin_t[:, 0:1])
            nc.sync.dma_start(out[:, c * W:(c + 1) * W], out_t[:])

        def final_pair(step):
            g, turn = divmod(step - FINAL_LAG, GROUP)
            if g < 0 or turn >= 2:
                return ()
            return (g * GROUP + 2 * turn, g * GROUP + 2 * turn + 1)

        for c in (0, 1):
            new_operands(c)
        for cb in range(CB):
            for c in (0, 1):
                make_difference(c, slice(cb, cb + 1))
                make_product(c, slice(cb, cb + 1))
            if cb == 0:
                for c in (0, 1):
                    nc.scalar.activation(operands[c]["xs_sq"][:, cb, :], operands[c]["xs"][:, cb, :], ACT.Square)
                for branch in branches:
                    first_layer_block(0, branch, 0)
        edge_t = load(nc.sync, [P, N], BF16, edge_attr, "edge_t")
        for step in range(CHUNKS - 1):
            if step + 3 < CHUNKS:
                fetch_xd(step + 3)
            def cosines_now():
                dot = group_products(step // GROUP, vector_is_free=False)
                group_norms(step // GROUP)
                group_cosines(step // GROUP, dot)

            if step + 2 < CHUNKS:
                make_operands(step + 2, between=cosines_now if step % GROUP == GROUP - 1 else None)
            if step - 2 >= CHUNKS - GROUP:
                open_final(step - 2)
            first_layer(step, branches[0])
            first_layer(step, branches[1])
            if step >= 1:
                second_layer(step - 1, 2)
            for c in final_pair(step):
                close_final(c)
            for c in final_pair(step + 1):
                open_final(c)
            first_layer(step, branches[2])
            second_layer(step, 0)
            second_layer(step, 1)
        last = CHUNKS - 1
        open_final(last - 2)
        first_layer(last, branches[0])
        first_layer(last, branches[1])
        second_layer(last - 1, 2)
        group_norms(last // GROUP)
        second_layer(last, 0, by_vector=True)
        first_layer(last, branches[2], by_vector=True)
        group_cosines(last // GROUP, group_products(last // GROUP, vector_is_free=True))
        second_layer(last, 1, by_vector=True)
        open_final(last - 1)
        second_layer(last, 2, by_vector=True)
        for c in range(last - 3, last):
            close_final(c)
        open_final(last)
        close_final(last)
